import numpy as np
import ml_dtypes


def mxq(x, axis, fmt="e4m3"):
    dtype, down = {"e4m3": (ml_dtypes.float8_e4m3fn, 7), "e5m2": (ml_dtypes.float8_e5m2, 14)}[fmt]
    v = np.moveaxis(np.asarray(x, np.float32).astype(ml_dtypes.bfloat16).astype(np.float64), axis, -1)
    blocks = v.reshape(v.shape[:-1] + (-1, 32))
    amax = np.abs(blocks).max(-1, keepdims=True)
    byte = np.maximum(np.where(amax > 0, np.frexp(amax)[1] - 1 + 127, 0) - down, 1)
    scale = np.exp2(byte - 127.0)
    codes = (blocks / scale).astype(np.float32).astype(dtype).astype(np.float64)
    return np.moveaxis((codes * scale).reshape(v.shape), -1, axis)


WIDE = False


def mx_kscale(k):
    if not WIDE:
        return np.ones(k)
    levels = np.array([10, -10, 5, -5, 0])
    a = np.random.permutation(np.resize(levels, k // 512 * 4)).reshape(k // 512, 4)
    idx = np.arange(k)
    return np.exp2(a[idx // 512, idx % 128 // 32])


BF16 = ml_dtypes.bfloat16


def bf(x):
    return np.asarray(x, np.float32).astype(BF16)


def f64(x):
    return np.asarray(x).astype(np.float64)


B, I, O, NK, ORDER = 3584, 32, 128, 19, 3
K = NK - ORDER


def silu(v):
    return v / (1.0 + np.exp(-v))


def make_knots():
    return np.linspace(-1.0 - 2.0 / NK, 1.0 + 2.0 / NK, NK)


def bspline_bases(t, knots, order):
    tb = t[:, None]
    b = ((knots[:-1] <= tb) & (knots[1:] > tb)).astype(np.float64)
    for k in range(1, order):
        left = (tb - knots[:-k - 1]) / (knots[k:-1] - knots[:-k - 1]) * b[:, :-1]
        right = (knots[k + 1:] - tb) / (knots[k + 1:] - knots[1:-k]) * b[:, 1:]
        b = left + right
    return b


def setup_inputs():
    s = mx_kscale(I * K)
    sb = np.repeat(s.reshape(-1, 32)[:, 0], 32).reshape(I, K)
    loud = sb >= max(2.0, sb.max() / 4.0)
    dead = np.broadcast_to(make_knots()[:K] >= -0.09, (I, K))
    f = loud.any(axis=1)
    x = np.random.uniform(-1.0, 1.0, (B, I))
    x[:, f] = -0.1 - 0.9 * np.abs(x[:, f])
    p = np.random.standard_normal((O, I, K)) * 1.5 / np.sqrt(I)
    p = np.where(loud & dead, p * sb * sb, np.where(loud, 0.0, p))
    return {"x": bf(x),
            "spline_parameters": bf(p),
            "w_b": bf((1.0 + 0.1 * np.random.standard_normal(1)) / np.sqrt(I)),
            "w_s": bf(1.0 + 0.1 * np.random.standard_normal(1))}


def reference(x, spline_parameters, w_b, w_s):
    x = f64(x)
    knots = np.linspace(-1.0 - 2.0 / NK, 1.0 + 2.0 / NK, NK)
    bases = bspline_bases(x.reshape(-1), knots, ORDER)
    bases = bases.reshape(B, I * K)
    p = f64(spline_parameters).reshape(O, I * K)
    splines = mxq(bases, 1, "e4m3") @ mxq(p, 1, "e4m3").T
    silu_sum = np.sum(silu(x), axis=-1, keepdims=True)
    return f64(w_b) * silu_sum + f64(w_s) * splines

@@ -1,0 +1,184 @@
+from contextlib import ExitStack
+import math
+
+import concourse.masks as masks
+import concourse.mybir as mybir
+
+F32 = mybir.dt.float32
+BF16 = mybir.dt.bfloat16
+U32 = mybir.dt.uint32
+U8 = mybir.dt.uint8
+FP8X4 = mybir.dt.float8_e4m3fn_x4
+ACT = mybir.ActivationFunctionType
+ALU = mybir.AluOpType
+
+P = 128
+BATCH, FEATURES, OUTS, BASES = 3584, 32, 128, 16
+ROWS = BATCH // P
+CHUNK = 4
+PAIRS = FEATURES // 2
+RES = 4
+CAND = FEATURES * RES
+KNOTS_PER_UNIT = 57.0 / 7.0
+ROUND_MAGIC = 12582912.0
+
+FLOPS = 2 * BATCH * FEATURES * BASES * OUTS
+
+
+def tile_bsplinekanlayer_s_kernel(tc, x, spline_parameters, w_b, w_s, out):
+    nc = tc.nc
+    x_rows = x.rearrange("(p t) i -> p t i", t=ROWS)
+    out_rows = out.rearrange("(p t) o -> p t o", t=ROWS)
+
+    with ExitStack() as ctx:
+        keep = ctx.enter_context(tc.tile_pool(name="keep", bufs=1))
+        work = ctx.enter_context(tc.tile_pool(name="work", bufs=3))
+        psum_words = ctx.enter_context(tc.psum_pool(name="psum_words", bufs=4))
+        psum_acc = ctx.enter_context(tc.psum_pool(name="psum_acc", bufs=2))
+        psum_par = ctx.enter_context(tc.psum_pool(name="psum_par", bufs=1))
+
+        x_sb = keep.tile([P, ROWS, FEATURES], BF16)
+        nc.sync.dma_start(out=x_sb[:], in_=x_rows)
+        par_sb = keep.tile([P, FEATURES * BASES], BF16)
+        nc.sync.dma_start(out=par_sb[:], in_=spline_parameters.rearrange("o i k -> o (i k)"))
+        wb_bf = keep.tile([P, 1], BF16)
+        nc.scalar.dma_start(out=wb_bf[:], in_=w_b.partition_broadcast(P))
+        ws_bf = keep.tile([P, 1], BF16)
+        nc.scalar.dma_start(out=ws_bf[:], in_=w_s.partition_broadcast(P))
+
+        ident = keep.tile([P, P], F32)
+        masks.make_identity(nc, ident[:])
+
+        silu = keep.tile([P, ROWS, FEATURES], F32)
+        nc.scalar.activation(out=silu[:], in_=x_sb[:], func=ACT.Silu)
+        silu_sum = keep.tile([P, ROWS], F32)
+        nc.vector.tensor_reduce(out=silu_sum[:], in_=silu[:], axis=mybir.AxisListType.X, op=ALU.add)
+        wb = keep.tile([P, 1], F32)
+        nc.vector.tensor_copy(out=wb[:], in_=wb_bf[:])
+        ws = keep.tile([P, 1], F32)
+        nc.vector.tensor_copy(out=ws[:], in_=ws_bf[:])
+        base_term = keep.tile([P, ROWS], F32)
+        nc.vector.tensor_scalar(
+            out=base_term[:], in0=silu_sum[:], scalar1=wb[:, 0:1], scalar2=None, op0=ALU.mult
+        )
+
+        par_pairs = keep.tile([P, 2 * P * 2], BF16)
+        par_src = par_sb[:].rearrange("o (q l u m) -> o u q m l", q=PAIRS, l=2, u=2, m=8)
+        par_dst = par_pairs[:].rearrange("o (u q m l) -> o u q m l", u=2, q=PAIRS, m=8, l=2)
+        for u in range(2):
+            nc.vector.tensor_copy(out=par_dst[:, u], in_=par_src[:, u])
+        par_t = psum_par.tile([P, 2, OUTS], F32)
+        for u in range(2):
+            nc.tensor.transpose(par_t[:, u, :], par_pairs[:].bitcast(F32)[:, u * P : (u + 1) * P], ident[:])
+        par_grouped = keep.tile([P, OUTS * 4], BF16, align_bytes=64)
+        nc.vector.tensor_copy(
+            out=par_grouped[:].bitcast(F32).rearrange("p (o u) -> p o u", u=2),
+            in_=par_t[:].rearrange("p u o -> p o u"),
+        )
+        par_codes = keep.tile([P, OUTS], U32, align_bytes=64)
+        par_scales = keep.tile([P, OUTS], U8, align_bytes=64)
+        nc.vector.quantize_mx(out=par_codes[:].bitcast(FP8X4), scales=par_scales[:], in_=par_grouped[:])
+
+        for first in range(0, ROWS, CHUNK):
+            rows = slice(first, first + CHUNK)
+            n = CHUNK * CAND
+
+            pos = work.tile([P, RES, CHUNK, FEATURES], F32)
+            for r in range(RES):
+                nc.scalar.activation(
+                    out=pos[:, r],
+                    in_=x_sb[:, rows, :],
+                    func=ACT.Identity,
+                    scale=KNOTS_PER_UNIT / 4.0,
+                    bias=(7.5 - r) / 4.0,
+                )
+            pos_v = pos[:].rearrange("p r c (q l) -> p (c q) r l", l=2)
+
+            which = work.tile([P, n], BF16)
+            nc.vector.tensor_scalar(
+                out=which[:].rearrange("p (a r l) -> p a r l", r=RES, l=2),
+                in0=pos_v,
+                scalar1=ROUND_MAGIC,
+                scalar2=ROUND_MAGIC,
+                op0=ALU.add,
+                op1=ALU.subtract,
+            )
+            off = work.tile([P, n], F32)
+            nc.vector.tensor_tensor(
+                out=off[:].rearrange("p (a r l) -> p a r l", r=RES, l=2),
+                in0=pos_v,
+                in1=which[:].rearrange("p (a r l) -> p a r l", r=RES, l=2),
+                op=ALU.subtract,
+            )
+            dist = work.tile([P, n], F32)
+            nc.scalar.activation(out=dist[:], in_=off[:], func=ACT.Abs, scale=4.0)
+            wide = work.tile([P, n], F32)
+            nc.scalar.activation(out=wide[:], in_=dist[:], func=ACT.Relu, scale=-1.0, bias=1.5)
+            narrow = work.tile([P, n], F32)
+            nc.scalar.activation(out=narrow[:], in_=dist[:], func=ACT.Relu, scale=-1.0, bias=0.5)
+            wide_sq = work.tile([P, n], F32)
+            nc.scalar.activation(out=wide_sq[:], in_=wide[:], func=ACT.Square, scale=math.sqrt(0.5))
+            narrow_sq = work.tile([P, n], F32)
+            nc.scalar.activation(out=narrow_sq[:], in_=narrow[:], func=ACT.Square, scale=math.sqrt(1.5))
+            value = work.tile([P, n], BF16)
+            nc.vector.tensor_tensor(out=value[:], in0=wide_sq[:], in1=narrow_sq[:], op=ALU.subtract)
+
+            hit = work.tile([P, RES, n], BF16)
+            bases = work.tile([P, CHUNK * FEATURES * BASES], BF16)
+            bases_v = bases[:].rearrange(
+                "p (c u q t m) -> p c u q t m", c=CHUNK, u=2, q=PAIRS, t=2, m=8
+            )
+            for s in range(4):
+                nc.vector.tensor_scalar(
+                    out=hit[:, s, :], in0=which[:], scalar1=float(s), scalar2=None, op0=ALU.is_equal
+                )
+                nc.vector.tensor_tensor(
+                    out=bases_v[:, :, s // 2, :, s % 2, :],
+                    in0=hit[:, s, :].rearrange("p (c q m) -> p c q m", c=CHUNK, q=PAIRS),
+                    in1=value[:].rearrange("p (c q m) -> p c q m", c=CHUNK, q=PAIRS),
+                    op=ALU.mult,
+                )
+
+            grouped = work.tile([P, CHUNK * P * 4], BF16, align_bytes=64)
+            grouped_v = grouped[:].bitcast(F32).rearrange("p (b u) -> p b u", u=2)
+            bases_w = bases[:].bitcast(F32)
+            for g in range(CHUNK // 2):
+                words = psum_words.tile([P, 2, 2 * P], F32)
+                for h in range(2):
+                    for u in range(2):
+                        col = ((2 * g + h) * 2 + u) * P
+                        nc.tensor.transpose(
+                            words[:, u, h * P : (h + 1) * P], bases_w[:, col : col + P], ident[:]
+                        )
+                nc.scalar.copy(
+                    out=grouped_v[:, g * 2 * P : (g + 1) * 2 * P, :],
+                    in_=words[:].rearrange("p u b -> p b u"),
+                )
+
+            codes = work.tile([P, CHUNK * P], U32, align_bytes=64)
+            scales = work.tile([P, CHUNK * P], U8, align_bytes=64)
+            nc.vector.quantize_mx(out=codes[:].bitcast(FP8X4), scales=scales[:], in_=grouped[:])
+
+            acc = psum_acc.tile([P, CHUNK, OUTS], F32)
+            for c in range(CHUNK):
+                cols = slice(c * P, (c + 1) * P)
+                nc.tensor.matmul_mx(
+                    out=acc[:, c, :],
+                    lhsT=codes[:, cols].bitcast(FP8X4),
+                    lhsT_scale=scales[:, cols],
+                    rhs=par_codes[:].bitcast(FP8X4),
+                    rhs_scale=par_scales[:],
+                    start=True,
+                    stop=True,
+                )
+
+            result = work.tile([P, CHUNK, OUTS], F32)
+            nc.vector.scalar_tensor_tensor(
+                out=result[:],
+                in0=acc[:],
+                scalar=ws[:, 0:1],
+                in1=base_term[:, rows].unsqueeze(2).to_broadcast([P, CHUNK, OUTS]),
+                op0=ALU.mult,
+                op1=ALU.add,
+            )
+            nc.sync.dma_start(out=out_rows[:, rows, :], in_=result[:])

@@ -16,9 +16,10 @@ P = 128
 BATCH, FEATURES, OUTS, BASES = 3584, 32, 128, 16
 ROWS = BATCH // P
 CHUNK = 4
+CHUNKS = ROWS // CHUNK
 PAIRS = FEATURES // 2
 RES = 4
-CAND = FEATURES * RES
+N = CHUNK * FEATURES * RES
 KNOTS_PER_UNIT = 57.0 / 7.0
 ROUND_MAGIC = 12582912.0
 
@@ -36,134 +37,175 @@ def tile_bsplinekanlayer_s_kernel(tc, x, spline_parameters, w_b, w_s, out):
         psum_words = ctx.enter_context(tc.psum_pool(name="psum_words", bufs=4))
         psum_acc = ctx.enter_context(tc.psum_pool(name="psum_acc", bufs=2))
         psum_par = ctx.enter_context(tc.psum_pool(name="psum_par", bufs=1))
+        ctx.enter_context(tc.manual_schedule())
 
         x_sb = keep.tile([P, ROWS, FEATURES], BF16)
         nc.sync.dma_start(out=x_sb[:], in_=x_rows)
         par_sb = keep.tile([P, FEATURES * BASES], BF16)
         nc.sync.dma_start(out=par_sb[:], in_=spline_parameters.rearrange("o i k -> o (i k)"))
         wb_bf = keep.tile([P, 1], BF16)
-        nc.scalar.dma_start(out=wb_bf[:], in_=w_b.partition_broadcast(P))
+        nc.sync.dma_start(out=wb_bf[:], in_=w_b.partition_broadcast(P))
         ws_bf = keep.tile([P, 1], BF16)
-        nc.scalar.dma_start(out=ws_bf[:], in_=w_s.partition_broadcast(P))
+        nc.sync.dma_start(out=ws_bf[:], in_=w_s.partition_broadcast(P))
 
         ident = keep.tile([P, P], F32)
         masks.make_identity(nc, ident[:])
 
-        silu = keep.tile([P, ROWS, FEATURES], F32)
-        nc.scalar.activation(out=silu[:], in_=x_sb[:], func=ACT.Silu)
-        silu_sum = keep.tile([P, ROWS], F32)
-        nc.vector.tensor_reduce(out=silu_sum[:], in_=silu[:], axis=mybir.AxisListType.X, op=ALU.add)
-        wb = keep.tile([P, 1], F32)
-        nc.vector.tensor_copy(out=wb[:], in_=wb_bf[:])
-        ws = keep.tile([P, 1], F32)
-        nc.vector.tensor_copy(out=ws[:], in_=ws_bf[:])
-        base_term = keep.tile([P, ROWS], F32)
-        nc.vector.tensor_scalar(
-            out=base_term[:], in0=silu_sum[:], scalar1=wb[:, 0:1], scalar2=None, op0=ALU.mult
-        )
+        warm = keep.tile([P, 1], F32)
+        nc.vector.memset(warm[:], 0.0)
+        nc.scalar.activation(out=warm[:], in_=warm[:], func=ACT.Abs)
 
-        par_pairs = keep.tile([P, 2 * P * 2], BF16)
-        par_src = par_sb[:].rearrange("o (q l u m) -> o u q m l", q=PAIRS, l=2, u=2, m=8)
-        par_dst = par_pairs[:].rearrange("o (u q m l) -> o u q m l", u=2, q=PAIRS, m=8, l=2)
-        for u in range(2):
-            nc.vector.tensor_copy(out=par_dst[:, u], in_=par_src[:, u])
-        par_t = psum_par.tile([P, 2, OUTS], F32)
-        for u in range(2):
-            nc.tensor.transpose(par_t[:, u, :], par_pairs[:].bitcast(F32)[:, u * P : (u + 1) * P], ident[:])
-        par_grouped = keep.tile([P, OUTS * 4], BF16, align_bytes=64)
-        nc.vector.tensor_copy(
-            out=par_grouped[:].bitcast(F32).rearrange("p (o u) -> p o u", u=2),
-            in_=par_t[:].rearrange("p u o -> p o u"),
-        )
+        base_term = keep.tile([P, ROWS], F32)
+        ws = keep.tile([P, 1], F32)
         par_codes = keep.tile([P, OUTS], U32, align_bytes=64)
         par_scales = keep.tile([P, OUTS], U8, align_bytes=64)
-        nc.vector.quantize_mx(out=par_codes[:].bitcast(FP8X4), scales=par_scales[:], in_=par_grouped[:])
 
-        for first in range(0, ROWS, CHUNK):
-            rows = slice(first, first + CHUNK)
-            n = CHUNK * CAND
+        tanh = keep.tile([P, ROWS, FEATURES], F32)
 
+        def half_tanh():
+            nc.scalar.activation(out=tanh[:], in_=x_sb[:], func=ACT.Tanh, scale=0.5)
+
+        def base_path():
+            twice_silu = keep.tile([P, ROWS, FEATURES], F32)
+            nc.vector.scalar_tensor_tensor(
+                out=twice_silu[:], in0=tanh[:], scalar=1.0, in1=x_sb[:], op0=ALU.add, op1=ALU.mult
+            )
+            twice_sum = keep.tile([P, ROWS], F32)
+            nc.vector.tensor_reduce(
+                out=twice_sum[:], in_=twice_silu[:], axis=mybir.AxisListType.X, op=ALU.add
+            )
+            wb = keep.tile([P, 1], F32)
+            nc.vector.tensor_copy(out=wb[:], in_=wb_bf[:])
+            nc.vector.tensor_copy(out=ws[:], in_=ws_bf[:])
+            nc.vector.tensor_scalar(
+                out=base_term[:], in0=twice_sum[:], scalar1=wb[:, 0:1], scalar2=0.5, op0=ALU.mult, op1=ALU.mult
+            )
+
+        par_t = psum_par.tile([P, 2, OUTS], F32)
+
+        def transpose_parameters():
+            par_pairs = keep.tile([P, 2 * P * 2], BF16)
+            par_src = par_sb[:].rearrange("o (q l u m) -> o u q m l", q=PAIRS, l=2, u=2, m=8)
+            par_dst = par_pairs[:].rearrange("o (u q m l) -> o u q m l", u=2, q=PAIRS, m=8, l=2)
+            for u in range(2):
+                nc.vector.tensor_copy(out=par_dst[:, u], in_=par_src[:, u])
+            for u in range(2):
+                nc.tensor.transpose(
+                    par_t[:, u, :], par_pairs[:].bitcast(F32)[:, u * P : (u + 1) * P], ident[:]
+                )
+
+        def quantise_parameters():
+            par_grouped = keep.tile([P, OUTS * 4], BF16, align_bytes=64)
+            nc.vector.tensor_copy(
+                out=par_grouped[:].bitcast(F32).rearrange("p (o u) -> p o u", u=2),
+                in_=par_t[:].rearrange("p u o -> p o u"),
+            )
+            nc.vector.quantize_mx(
+                out=par_codes[:].bitcast(FP8X4), scales=par_scales[:], in_=par_grouped[:]
+            )
+
+        pos_of, which_of, off_of, squares_of, words_of, grouped_of, acc_of = {}, {}, {}, {}, {}, {}, {}
+
+        def by_class(flat):
+            return flat.rearrange("p (a r l) -> p a r l", r=RES, l=2)
+
+        def by_pair(flat):
+            return flat.rearrange("p (c q m) -> p c q m", c=CHUNK, q=PAIRS)
+
+        def positions(c):
             pos = work.tile([P, RES, CHUNK, FEATURES], F32)
             for r in range(RES):
                 nc.scalar.activation(
                     out=pos[:, r],
-                    in_=x_sb[:, rows, :],
+                    in_=x_sb[:, c * CHUNK : (c + 1) * CHUNK, :],
                     func=ACT.Identity,
                     scale=KNOTS_PER_UNIT / 4.0,
                     bias=(7.5 - r) / 4.0,
                 )
-            pos_v = pos[:].rearrange("p r c (q l) -> p (c q) r l", l=2)
+            pos_of[c] = pos
 
-            which = work.tile([P, n], BF16)
+        def nearest(c):
+            pos_v = pos_of[c][:].rearrange("p r c (q l) -> p (c q) r l", l=2)
+            which = work.tile([P, N], BF16)
             nc.vector.tensor_scalar(
-                out=which[:].rearrange("p (a r l) -> p a r l", r=RES, l=2),
+                out=by_class(which[:]),
                 in0=pos_v,
                 scalar1=ROUND_MAGIC,
                 scalar2=ROUND_MAGIC,
                 op0=ALU.add,
                 op1=ALU.subtract,
             )
-            off = work.tile([P, n], F32)
-            nc.vector.tensor_tensor(
-                out=off[:].rearrange("p (a r l) -> p a r l", r=RES, l=2),
-                in0=pos_v,
-                in1=which[:].rearrange("p (a r l) -> p a r l", r=RES, l=2),
-                op=ALU.subtract,
-            )
-            dist = work.tile([P, n], F32)
-            nc.scalar.activation(out=dist[:], in_=off[:], func=ACT.Abs, scale=4.0)
-            wide = work.tile([P, n], F32)
-            nc.scalar.activation(out=wide[:], in_=dist[:], func=ACT.Relu, scale=-1.0, bias=1.5)
-            narrow = work.tile([P, n], F32)
-            nc.scalar.activation(out=narrow[:], in_=dist[:], func=ACT.Relu, scale=-1.0, bias=0.5)
-            wide_sq = work.tile([P, n], F32)
-            nc.scalar.activation(out=wide_sq[:], in_=wide[:], func=ACT.Square, scale=math.sqrt(0.5))
-            narrow_sq = work.tile([P, n], F32)
-            nc.scalar.activation(out=narrow_sq[:], in_=narrow[:], func=ACT.Square, scale=math.sqrt(1.5))
-            value = work.tile([P, n], BF16)
-            nc.vector.tensor_tensor(out=value[:], in0=wide_sq[:], in1=narrow_sq[:], op=ALU.subtract)
+            off = work.tile([P, N], F32)
+            nc.vector.tensor_tensor(out=by_class(off[:]), in0=pos_v, in1=by_class(which[:]), op=ALU.subtract)
+            which_of[c] = which
+            off_of[c] = off
 
-            hit = work.tile([P, RES, n], BF16)
+        def squares(c):
+            dist = work.tile([P, N], F32)
+            nc.scalar.activation(out=dist[:], in_=off_of[c][:], func=ACT.Abs, scale=4.0)
+            wide = work.tile([P, N], F32)
+            nc.scalar.activation(out=wide[:], in_=dist[:], func=ACT.Relu, scale=-1.0, bias=1.5)
+            narrow = work.tile([P, N], F32)
+            nc.scalar.activation(out=narrow[:], in_=dist[:], func=ACT.Relu, scale=-1.0, bias=0.5)
+            wide_sq = work.tile([P, N], F32)
+            nc.scalar.activation(out=wide_sq[:], in_=wide[:], func=ACT.Square, scale=math.sqrt(0.5))
+            narrow_sq = work.tile([P, N], F32)
+            nc.scalar.activation(out=narrow_sq[:], in_=narrow[:], func=ACT.Square, scale=math.sqrt(1.5))
+            squares_of[c] = (wide_sq, narrow_sq)
+
+        def spread(c):
+            wide_sq, narrow_sq = squares_of[c]
+            which = which_of[c]
+            value = work.tile([P, N], BF16)
+            nc.vector.tensor_tensor(out=value[:], in0=wide_sq[:], in1=narrow_sq[:], op=ALU.subtract)
+            hit = work.tile([P, RES, N], BF16)
             bases = work.tile([P, CHUNK * FEATURES * BASES], BF16)
-            bases_v = bases[:].rearrange(
-                "p (c u q t m) -> p c u q t m", c=CHUNK, u=2, q=PAIRS, t=2, m=8
-            )
+            bases_v = bases[:].rearrange("p (c u q t m) -> p c u q t m", c=CHUNK, u=2, q=PAIRS, t=2, m=8)
             for s in range(4):
                 nc.vector.tensor_scalar(
                     out=hit[:, s, :], in0=which[:], scalar1=float(s), scalar2=None, op0=ALU.is_equal
                 )
+            for s in range(4):
                 nc.vector.tensor_tensor(
                     out=bases_v[:, :, s // 2, :, s % 2, :],
-                    in0=hit[:, s, :].rearrange("p (c q m) -> p c q m", c=CHUNK, q=PAIRS),
-                    in1=value[:].rearrange("p (c q m) -> p c q m", c=CHUNK, q=PAIRS),
+                    in0=by_pair(hit[:, s, :]),
+                    in1=by_pair(value[:]),
                     op=ALU.mult,
                 )
-
-            grouped = work.tile([P, CHUNK * P * 4], BF16, align_bytes=64)
-            grouped_v = grouped[:].bitcast(F32).rearrange("p (b u) -> p b u", u=2)
             bases_w = bases[:].bitcast(F32)
+            banks = []
             for g in range(CHUNK // 2):
                 words = psum_words.tile([P, 2, 2 * P], F32)
-                for h in range(2):
-                    for u in range(2):
-                        col = ((2 * g + h) * 2 + u) * P
-                        nc.tensor.transpose(
-                            words[:, u, h * P : (h + 1) * P], bases_w[:, col : col + P], ident[:]
-                        )
+                banks.append(words)
+            for row in range(CHUNK):
+                for u in range(2):
+                    col = (row * 2 + u) * P
+                    nc.tensor.transpose(
+                        banks[row // 2][:, u, (row % 2) * P : (row % 2 + 1) * P],
+                        bases_w[:, col : col + P],
+                        ident[:],
+                    )
+            words_of[c] = banks
+
+        def regroup(c):
+            grouped = work.tile([P, CHUNK * P * 4], BF16, align_bytes=64)
+            grouped_v = grouped[:].bitcast(F32).rearrange("p (b u) -> p b u", u=2)
+            for g in range(CHUNK // 2):
                 nc.scalar.copy(
                     out=grouped_v[:, g * 2 * P : (g + 1) * 2 * P, :],
-                    in_=words[:].rearrange("p u b -> p b u"),
+                    in_=words_of[c][g][:].rearrange("p u b -> p b u"),
                 )
+            grouped_of[c] = grouped
 
+        def multiply(c):
             codes = work.tile([P, CHUNK * P], U32, align_bytes=64)
             scales = work.tile([P, CHUNK * P], U8, align_bytes=64)
-            nc.vector.quantize_mx(out=codes[:].bitcast(FP8X4), scales=scales[:], in_=grouped[:])
-
+            nc.vector.quantize_mx(out=codes[:].bitcast(FP8X4), scales=scales[:], in_=grouped_of[c][:])
             acc = psum_acc.tile([P, CHUNK, OUTS], F32)
-            for c in range(CHUNK):
-                cols = slice(c * P, (c + 1) * P)
+            for row in range(CHUNK):
+                cols = slice(row * P, (row + 1) * P)
                 nc.tensor.matmul_mx(
-                    out=acc[:, c, :],
+                    out=acc[:, row, :],
                     lhsT=codes[:, cols].bitcast(FP8X4),
                     lhsT_scale=scales[:, cols],
                     rhs=par_codes[:].bitcast(FP8X4),
@@ -171,14 +213,40 @@ def tile_bsplinekanlayer_s_kernel(tc, x, spline_parameters, w_b, w_s, out):
                     start=True,
                     stop=True,
                 )
+            acc_of[c] = acc
 
+        def finish(c):
+            rows = slice(c * CHUNK, (c + 1) * CHUNK)
             result = work.tile([P, CHUNK, OUTS], F32)
             nc.vector.scalar_tensor_tensor(
                 out=result[:],
-                in0=acc[:],
+                in0=acc_of[c][:],
                 scalar=ws[:, 0:1],
                 in1=base_term[:, rows].unsqueeze(2).to_broadcast([P, CHUNK, OUTS]),
                 op0=ALU.mult,
                 op1=ALU.add,
             )
             nc.sync.dma_start(out=out_rows[:, rows, :], in_=result[:])
+
+        def run(stage, c):
+            if 0 <= c < CHUNKS:
+                stage(c)
+
+        def step(t):
+            run(spread, t - 1)
+            run(squares, t)
+            run(positions, t + 2)
+            run(regroup, t - 1)
+            run(nearest, t + 1)
+            run(multiply, t - 2)
+            run(finish, t - 3)
+
+        step(-2)
+        step(-1)
+        half_tanh()
+        transpose_parameters()
+        step(0)
+        quantise_parameters()
+        base_path()
+        for t in range(1, CHUNKS + 3):
+            step(t)

@@ -40,7 +40,8 @@ def tile_bsplinekanlayer_s_kernel(tc, x, spline_parameters, w_b, w_s, out):
         ctx.enter_context(tc.manual_schedule())
 
         x_sb = keep.tile([P, ROWS, FEATURES], BF16)
-        nc.sync.dma_start(out=x_sb[:], in_=x_rows)
+        nc.sync.dma_start(out=x_sb[:, 0 : 2 * CHUNK, :], in_=x_rows[:, 0 : 2 * CHUNK, :])
+        nc.sync.dma_start(out=x_sb[:, 2 * CHUNK : ROWS, :], in_=x_rows[:, 2 * CHUNK : ROWS, :])
         par_sb = keep.tile([P, FEATURES * BASES], BF16)
         nc.sync.dma_start(out=par_sb[:], in_=spline_parameters.rearrange("o i k -> o (i k)"))
         wb_bf = keep.tile([P, 1], BF16)
@@ -104,7 +105,7 @@ def tile_bsplinekanlayer_s_kernel(tc, x, spline_parameters, w_b, w_s, out):
                 out=par_codes[:].bitcast(FP8X4), scales=par_scales[:], in_=par_grouped[:]
             )
 
-        pos_of, which_of, off_of, squares_of, words_of, grouped_of, acc_of = {}, {}, {}, {}, {}, {}, {}
+        pos_of, hit_of, off_of, squares_of, words_of, grouped_of, acc_of = {}, {}, {}, {}, {}, {}, {}
 
         def by_class(flat):
             return flat.rearrange("p (a r l) -> p a r l", r=RES, l=2)
@@ -135,18 +136,33 @@ def tile_bsplinekanlayer_s_kernel(tc, x, spline_parameters, w_b, w_s, out):
                 op0=ALU.add,
                 op1=ALU.subtract,
             )
-            off = work.tile([P, N], F32)
-            nc.vector.tensor_tensor(out=by_class(off[:]), in0=pos_v, in1=by_class(which[:]), op=ALU.subtract)
-            which_of[c] = which
+            off = work.tile([P, N // 2], F32)
+            nc.vector.tensor_tensor(
+                out=off[:].rearrange("p (a r l) -> p a r l", r=2, l=2),
+                in0=pos_v[:, :, 0:2, :],
+                in1=by_class(which[:])[:, :, 0:2, :],
+                op=ALU.subtract,
+            )
+            hit = work.tile([P, RES, N], BF16)
+            for s in range(4):
+                nc.vector.tensor_scalar(
+                    out=hit[:, s, :], in0=which[:], scalar1=float(s), scalar2=None, op0=ALU.is_equal
+                )
+            hit_of[c] = hit
             off_of[c] = off
 
         def squares(c):
-            dist = work.tile([P, N], F32)
+            dist = work.tile([P, N // 2], F32)
             nc.scalar.activation(out=dist[:], in_=off_of[c][:], func=ACT.Abs, scale=4.0)
+            dist_v = dist[:].rearrange("p (a m) -> p a m", m=4)
             wide = work.tile([P, N], F32)
-            nc.scalar.activation(out=wide[:], in_=dist[:], func=ACT.Relu, scale=-1.0, bias=1.5)
             narrow = work.tile([P, N], F32)
-            nc.scalar.activation(out=narrow[:], in_=dist[:], func=ACT.Relu, scale=-1.0, bias=0.5)
+            wide_v = wide[:].rearrange("p (a h m) -> p a h m", h=2, m=4)
+            narrow_v = narrow[:].rearrange("p (a h m) -> p a h m", h=2, m=4)
+            nc.scalar.activation(out=wide_v[:, :, 0, :], in_=dist_v, func=ACT.Relu, scale=-1.0, bias=1.5)
+            nc.scalar.activation(out=wide_v[:, :, 1, :], in_=dist_v, func=ACT.Relu, scale=1.0, bias=-0.5)
+            nc.scalar.activation(out=narrow_v[:, :, 0, :], in_=dist_v, func=ACT.Relu, scale=-1.0, bias=0.5)
+            nc.scalar.activation(out=narrow_v[:, :, 1, :], in_=dist_v, func=ACT.Relu, scale=1.0, bias=-1.5)
             wide_sq = work.tile([P, N], F32)
             nc.scalar.activation(out=wide_sq[:], in_=wide[:], func=ACT.Square, scale=math.sqrt(0.5))
             narrow_sq = work.tile([P, N], F32)
@@ -155,36 +171,30 @@ def tile_bsplinekanlayer_s_kernel(tc, x, spline_parameters, w_b, w_s, out):
 
         def spread(c):
             wide_sq, narrow_sq = squares_of[c]
-            which = which_of[c]
+            hit = hit_of[c]
             value = work.tile([P, N], BF16)
             nc.vector.tensor_tensor(out=value[:], in0=wide_sq[:], in1=narrow_sq[:], op=ALU.subtract)
-            hit = work.tile([P, RES, N], BF16)
             bases = work.tile([P, CHUNK * FEATURES * BASES], BF16)
             bases_v = bases[:].rearrange("p (c u q t m) -> p c u q t m", c=CHUNK, u=2, q=PAIRS, t=2, m=8)
-            for s in range(4):
-                nc.vector.tensor_scalar(
-                    out=hit[:, s, :], in0=which[:], scalar1=float(s), scalar2=None, op0=ALU.is_equal
-                )
-            for s in range(4):
-                nc.vector.tensor_tensor(
-                    out=bases_v[:, :, s // 2, :, s % 2, :],
-                    in0=by_pair(hit[:, s, :]),
-                    in1=by_pair(value[:]),
-                    op=ALU.mult,
-                )
             bases_w = bases[:].bitcast(F32)
             banks = []
             for g in range(CHUNK // 2):
-                words = psum_words.tile([P, 2, 2 * P], F32)
-                banks.append(words)
-            for row in range(CHUNK):
-                for u in range(2):
-                    col = (row * 2 + u) * P
-                    nc.tensor.transpose(
-                        banks[row // 2][:, u, (row % 2) * P : (row % 2 + 1) * P],
-                        bases_w[:, col : col + P],
-                        ident[:],
+                two = slice(2 * g, 2 * g + 2)
+                for s in range(4):
+                    nc.vector.tensor_tensor(
+                        out=bases_v[:, two, s // 2, :, s % 2, :],
+                        in0=by_pair(hit[:, s, :])[:, two],
+                        in1=by_pair(value[:])[:, two],
+                        op=ALU.mult,
                     )
+                words = psum_words.tile([P, 2, 2 * P], F32)
+                for h in range(2):
+                    for u in range(2):
+                        col = ((2 * g + h) * 2 + u) * P
+                        nc.tensor.transpose(
+                            words[:, u, h * P : (h + 1) * P], bases_w[:, col : col + P], ident[:]
+                        )
+                banks.append(words)
             words_of[c] = banks
 
         def regroup(c):
@@ -200,8 +210,14 @@ def tile_bsplinekanlayer_s_kernel(tc, x, spline_parameters, w_b, w_s, out):
         def multiply(c):
             codes = work.tile([P, CHUNK * P], U32, align_bytes=64)
             scales = work.tile([P, CHUNK * P], U8, align_bytes=64)
-            nc.vector.quantize_mx(out=codes[:].bitcast(FP8X4), scales=scales[:], in_=grouped_of[c][:])
             acc = psum_acc.tile([P, CHUNK, OUTS], F32)
+            for g in range(CHUNK // 2):
+                cols = slice(g * 2 * P, (g + 1) * 2 * P)
+                nc.vector.quantize_mx(
+                    out=codes[:, cols].bitcast(FP8X4),
+                    scales=scales[:, cols],
+                    in_=grouped_of[c][:, g * 8 * P : (g + 1) * 8 * P],
+                )
             for row in range(CHUNK):
                 cols = slice(row * P, (row + 1) * P)
                 nc.tensor.matmul_mx(

@@ -15,11 +15,11 @@ ALU = mybir.AluOpType
 P = 128
 BATCH, FEATURES, OUTS, BASES = 3584, 32, 128, 16
 ROWS = BATCH // P
-CHUNK = 4
-CHUNKS = ROWS // CHUNK
+CHUNK = 6
+CHUNKS = -(-ROWS // CHUNK)
 PAIRS = FEATURES // 2
 RES = 4
-N = CHUNK * FEATURES * RES
+CAND = FEATURES * RES
 KNOTS_PER_UNIT = 57.0 / 7.0
 ROUND_MAGIC = 12582912.0
 
@@ -35,15 +35,14 @@ def tile_bsplinekanlayer_s_kernel(tc, x, spline_parameters, w_b, w_s, out):
         keep = ctx.enter_context(tc.tile_pool(name="keep", bufs=1))
         work = ctx.enter_context(tc.tile_pool(name="work", bufs=3))
         psum_words = ctx.enter_context(tc.psum_pool(name="psum_words", bufs=4))
-        psum_acc = ctx.enter_context(tc.psum_pool(name="psum_acc", bufs=2))
-        psum_par = ctx.enter_context(tc.psum_pool(name="psum_par", bufs=1))
+        psum_acc = ctx.enter_context(tc.psum_pool(name="psum_acc", bufs=4))
         ctx.enter_context(tc.manual_schedule())
 
+        par_sb = keep.tile([P, FEATURES * BASES], BF16)
+        nc.scalar.dma_start(out=par_sb[:], in_=spline_parameters.rearrange("o i k -> o (i k)"))
         x_sb = keep.tile([P, ROWS, FEATURES], BF16)
         nc.sync.dma_start(out=x_sb[:, 0 : 2 * CHUNK, :], in_=x_rows[:, 0 : 2 * CHUNK, :])
         nc.sync.dma_start(out=x_sb[:, 2 * CHUNK : ROWS, :], in_=x_rows[:, 2 * CHUNK : ROWS, :])
-        par_sb = keep.tile([P, FEATURES * BASES], BF16)
-        nc.sync.dma_start(out=par_sb[:], in_=spline_parameters.rearrange("o i k -> o (i k)"))
         wb_bf = keep.tile([P, 1], BF16)
         nc.sync.dma_start(out=wb_bf[:], in_=w_b.partition_broadcast(P))
         ws_bf = keep.tile([P, 1], BF16)
@@ -60,8 +59,8 @@ def tile_bsplinekanlayer_s_kernel(tc, x, spline_parameters, w_b, w_s, out):
         ws = keep.tile([P, 1], F32)
         par_codes = keep.tile([P, OUTS], U32, align_bytes=64)
         par_scales = keep.tile([P, OUTS], U8, align_bytes=64)
-
         tanh = keep.tile([P, ROWS, FEATURES], F32)
+        par_t = psum_words.tile([P, 2, OUTS], F32, tag="words")
 
         def half_tanh():
             nc.scalar.activation(out=tanh[:], in_=x_sb[:], func=ACT.Tanh, scale=0.5)
@@ -81,8 +80,6 @@ def tile_bsplinekanlayer_s_kernel(tc, x, spline_parameters, w_b, w_s, out):
             nc.vector.tensor_scalar(
                 out=base_term[:], in0=twice_sum[:], scalar1=wb[:, 0:1], scalar2=0.5, op0=ALU.mult, op1=ALU.mult
             )
-
-        par_t = psum_par.tile([P, 2, OUTS], F32)
 
         def transpose_parameters():
             par_pairs = keep.tile([P, 2 * P * 2], BF16)
@@ -107,18 +104,25 @@ def tile_bsplinekanlayer_s_kernel(tc, x, spline_parameters, w_b, w_s, out):
 
         pos_of, hit_of, off_of, squares_of, words_of, grouped_of, acc_of = {}, {}, {}, {}, {}, {}, {}
 
+        def rows_of(c):
+            return min(CHUNK, ROWS - c * CHUNK)
+
         def by_class(flat):
             return flat.rearrange("p (a r l) -> p a r l", r=RES, l=2)
 
         def by_pair(flat):
-            return flat.rearrange("p (c q m) -> p c q m", c=CHUNK, q=PAIRS)
+            return flat.rearrange("p (c q m) -> p c q m", q=PAIRS, m=8)
+
+        def by_member(flat):
+            return flat.rearrange("p (c u q t m) -> p c u q t m", u=2, q=PAIRS, t=2, m=8)
 
         def positions(c):
-            pos = work.tile([P, RES, CHUNK, FEATURES], F32)
+            rows = rows_of(c)
+            pos = work.tile([P, RES, rows, FEATURES], F32)
             for r in range(RES):
                 nc.scalar.activation(
                     out=pos[:, r],
-                    in_=x_sb[:, c * CHUNK : (c + 1) * CHUNK, :],
+                    in_=x_sb[:, c * CHUNK : c * CHUNK + rows, :],
                     func=ACT.Identity,
                     scale=KNOTS_PER_UNIT / 4.0,
                     bias=(7.5 - r) / 4.0,
@@ -126,8 +130,9 @@ def tile_bsplinekanlayer_s_kernel(tc, x, spline_parameters, w_b, w_s, out):
             pos_of[c] = pos
 
         def nearest(c):
+            n = rows_of(c) * CAND
             pos_v = pos_of[c][:].rearrange("p r c (q l) -> p (c q) r l", l=2)
-            which = work.tile([P, N], BF16)
+            which = work.tile([P, n], BF16)
             nc.vector.tensor_scalar(
                 out=by_class(which[:]),
                 in0=pos_v,
@@ -136,55 +141,61 @@ def tile_bsplinekanlayer_s_kernel(tc, x, spline_parameters, w_b, w_s, out):
                 op0=ALU.add,
                 op1=ALU.subtract,
             )
-            off = work.tile([P, N // 2], F32)
+            off = work.tile([P, n // 2], F32)
             nc.vector.tensor_tensor(
                 out=off[:].rearrange("p (a r l) -> p a r l", r=2, l=2),
                 in0=pos_v[:, :, 0:2, :],
                 in1=by_class(which[:])[:, :, 0:2, :],
                 op=ALU.subtract,
             )
-            hit = work.tile([P, RES, N], BF16)
+            hit = work.tile([P, 4 * n], BF16)
             for s in range(4):
                 nc.vector.tensor_scalar(
-                    out=hit[:, s, :], in0=which[:], scalar1=float(s), scalar2=None, op0=ALU.is_equal
+                    out=by_member(hit[:])[:, :, s // 2, :, s % 2, :],
+                    in0=by_pair(which[:]),
+                    scalar1=float(s),
+                    scalar2=None,
+                    op0=ALU.is_equal,
                 )
             hit_of[c] = hit
             off_of[c] = off
 
         def squares(c):
-            dist = work.tile([P, N // 2], F32)
+            n = rows_of(c) * CAND
+            dist = work.tile([P, n // 2], F32)
             nc.scalar.activation(out=dist[:], in_=off_of[c][:], func=ACT.Abs, scale=4.0)
             dist_v = dist[:].rearrange("p (a m) -> p a m", m=4)
-            wide = work.tile([P, N], F32)
-            narrow = work.tile([P, N], F32)
+            wide = work.tile([P, n], F32)
+            narrow = work.tile([P, n], F32)
             wide_v = wide[:].rearrange("p (a h m) -> p a h m", h=2, m=4)
             narrow_v = narrow[:].rearrange("p (a h m) -> p a h m", h=2, m=4)
             nc.scalar.activation(out=wide_v[:, :, 0, :], in_=dist_v, func=ACT.Relu, scale=-1.0, bias=1.5)
             nc.scalar.activation(out=wide_v[:, :, 1, :], in_=dist_v, func=ACT.Relu, scale=1.0, bias=-0.5)
             nc.scalar.activation(out=narrow_v[:, :, 0, :], in_=dist_v, func=ACT.Relu, scale=-1.0, bias=0.5)
             nc.scalar.activation(out=narrow_v[:, :, 1, :], in_=dist_v, func=ACT.Relu, scale=1.0, bias=-1.5)
-            wide_sq = work.tile([P, N], F32)
+            wide_sq = work.tile([P, n], F32)
             nc.scalar.activation(out=wide_sq[:], in_=wide[:], func=ACT.Square, scale=math.sqrt(0.5))
-            narrow_sq = work.tile([P, N], F32)
+            narrow_sq = work.tile([P, n], F32)
             nc.scalar.activation(out=narrow_sq[:], in_=narrow[:], func=ACT.Square, scale=math.sqrt(1.5))
             squares_of[c] = (wide_sq, narrow_sq)
 
         def spread(c):
+            rows = rows_of(c)
+            n = rows * CAND
             wide_sq, narrow_sq = squares_of[c]
             hit = hit_of[c]
-            value = work.tile([P, N], BF16)
+            value = work.tile([P, n], BF16)
             nc.vector.tensor_tensor(out=value[:], in0=wide_sq[:], in1=narrow_sq[:], op=ALU.subtract)
-            bases = work.tile([P, CHUNK * FEATURES * BASES], BF16)
-            bases_v = bases[:].rearrange("p (c u q t m) -> p c u q t m", c=CHUNK, u=2, q=PAIRS, t=2, m=8)
+            bases = work.tile([P, 4 * n], BF16)
             bases_w = bases[:].bitcast(F32)
             banks = []
-            for g in range(CHUNK // 2):
+            for g in range(rows // 2):
                 two = slice(2 * g, 2 * g + 2)
-                for s in range(4):
+                for u in range(2):
                     nc.vector.tensor_tensor(
-                        out=bases_v[:, two, s // 2, :, s % 2, :],
-                        in0=by_pair(hit[:, s, :])[:, two],
-                        in1=by_pair(value[:])[:, two],
+                        out=by_member(bases[:])[:, two, u],
+                        in0=by_member(hit[:])[:, two, u],
+                        in1=by_pair(value[:])[:, two].unsqueeze(3).to_broadcast([P, 2, PAIRS, 2, 8]),
                         op=ALU.mult,
                     )
                 words = psum_words.tile([P, 2, 2 * P], F32)
@@ -198,9 +209,10 @@ def tile_bsplinekanlayer_s_kernel(tc, x, spline_parameters, w_b, w_s, out):
             words_of[c] = banks
 
         def regroup(c):
-            grouped = work.tile([P, CHUNK * P * 4], BF16, align_bytes=64)
+            rows = rows_of(c)
+            grouped = work.tile([P, rows * P * 4], BF16, align_bytes=64)
             grouped_v = grouped[:].bitcast(F32).rearrange("p (b u) -> p b u", u=2)
-            for g in range(CHUNK // 2):
+            for g in range(rows // 2):
                 nc.scalar.copy(
                     out=grouped_v[:, g * 2 * P : (g + 1) * 2 * P, :],
                     in_=words_of[c][g][:].rearrange("p u b -> p b u"),
@@ -208,41 +220,49 @@ def tile_bsplinekanlayer_s_kernel(tc, x, spline_parameters, w_b, w_s, out):
             grouped_of[c] = grouped
 
         def multiply(c):
-            codes = work.tile([P, CHUNK * P], U32, align_bytes=64)
-            scales = work.tile([P, CHUNK * P], U8, align_bytes=64)
-            acc = psum_acc.tile([P, CHUNK, OUTS], F32)
-            for g in range(CHUNK // 2):
+            rows = rows_of(c)
+            codes = work.tile([P, rows * P], U32, align_bytes=64)
+            scales = work.tile([P, rows * P], U8, align_bytes=64)
+            for g in range(rows // 2):
                 cols = slice(g * 2 * P, (g + 1) * 2 * P)
                 nc.vector.quantize_mx(
                     out=codes[:, cols].bitcast(FP8X4),
                     scales=scales[:, cols],
                     in_=grouped_of[c][:, g * 8 * P : (g + 1) * 8 * P],
                 )
-            for row in range(CHUNK):
-                cols = slice(row * P, (row + 1) * P)
-                nc.tensor.matmul_mx(
-                    out=acc[:, row, :],
-                    lhsT=codes[:, cols].bitcast(FP8X4),
-                    lhsT_scale=scales[:, cols],
-                    rhs=par_codes[:].bitcast(FP8X4),
-                    rhs_scale=par_scales[:],
-                    start=True,
-                    stop=True,
-                )
-            acc_of[c] = acc
+            accs = []
+            for first in range(0, rows, 4):
+                acc = psum_acc.tile([P, min(4, rows - first), OUTS], F32)
+                for row in range(first, min(first + 4, rows)):
+                    cols = slice(row * P, (row + 1) * P)
+                    nc.tensor.matmul_mx(
+                        out=acc[:, row - first, :],
+                        lhsT=codes[:, cols].bitcast(FP8X4),
+                        lhsT_scale=scales[:, cols],
+                        rhs=par_codes[:].bitcast(FP8X4),
+                        rhs_scale=par_scales[:],
+                        start=True,
+                        stop=True,
+                    )
+                accs.append(acc)
+            acc_of[c] = accs
 
         def finish(c):
-            rows = slice(c * CHUNK, (c + 1) * CHUNK)
-            result = work.tile([P, CHUNK, OUTS], F32)
-            nc.vector.scalar_tensor_tensor(
-                out=result[:],
-                in0=acc_of[c][:],
-                scalar=ws[:, 0:1],
-                in1=base_term[:, rows].unsqueeze(2).to_broadcast([P, CHUNK, OUTS]),
-                op0=ALU.mult,
-                op1=ALU.add,
-            )
-            nc.sync.dma_start(out=out_rows[:, rows, :], in_=result[:])
+            rows = rows_of(c)
+            result = work.tile([P, rows, OUTS], F32)
+            for a, acc in enumerate(acc_of[c]):
+                k = acc.shape[1]
+                nc.vector.scalar_tensor_tensor(
+                    out=result[:, 4 * a : 4 * a + k, :],
+                    in0=acc[:],
+                    scalar=ws[:, 0:1],
+                    in1=base_term[:, c * CHUNK + 4 * a : c * CHUNK + 4 * a + k]
+                    .unsqueeze(2)
+                    .to_broadcast([P, k, OUTS]),
+                    op0=ALU.mult,
+                    op1=ALU.add,
+                )
+            nc.sync.dma_start(out=out_rows[:, c * CHUNK : c * CHUNK + rows, :], in_=result[:])
 
         def run(stage, c):
             if 0 <= c < CHUNKS:
@@ -257,12 +277,12 @@ def tile_bsplinekanlayer_s_kernel(tc, x, spline_parameters, w_b, w_s, out):
             run(multiply, t - 2)
             run(finish, t - 3)
 
+        transpose_parameters()
         step(-2)
         step(-1)
         half_tanh()
-        transpose_parameters()
-        step(0)
         quantise_parameters()
+        step(0)
         base_path()
         for t in range(1, CHUNKS + 3):
             step(t)

@@ -70,13 +70,13 @@ def tile_bsplinekanlayer_s_kernel(tc, x, spline_parameters, w_b, w_s, out):
             nc.vector.scalar_tensor_tensor(
                 out=twice_silu[:], in0=tanh[:], scalar=1.0, in1=x_sb[:], op0=ALU.add, op1=ALU.mult
             )
+            wb = keep.tile([P, 1], F32)
+            nc.vector.tensor_copy(out=wb[:], in_=wb_bf[:])
+            nc.vector.tensor_copy(out=ws[:], in_=ws_bf[:])
             twice_sum = keep.tile([P, ROWS], F32)
             nc.vector.tensor_reduce(
                 out=twice_sum[:], in_=twice_silu[:], axis=mybir.AxisListType.X, op=ALU.add
             )
-            wb = keep.tile([P, 1], F32)
-            nc.vector.tensor_copy(out=wb[:], in_=wb_bf[:])
-            nc.vector.tensor_copy(out=ws[:], in_=ws_bf[:])
             nc.vector.tensor_scalar(
                 out=base_term[:], in0=twice_sum[:], scalar1=wb[:, 0:1], scalar2=0.5, op0=ALU.mult, op1=ALU.mult
             )
@@ -92,17 +92,21 @@ def tile_bsplinekanlayer_s_kernel(tc, x, spline_parameters, w_b, w_s, out):
                     par_t[:, u, :], par_pairs[:].bitcast(F32)[:, u * P : (u + 1) * P], ident[:]
                 )
 
-        def quantise_parameters():
-            par_grouped = keep.tile([P, OUTS * 4], BF16, align_bytes=64)
+        par_grouped = keep.tile([P, OUTS * 4], BF16, align_bytes=64)
+
+        def regroup_parameters():
             nc.vector.tensor_copy(
                 out=par_grouped[:].bitcast(F32).rearrange("p (o u) -> p o u", u=2),
                 in_=par_t[:].rearrange("p u o -> p o u"),
             )
+
+        def quantise_parameters():
             nc.vector.quantize_mx(
                 out=par_codes[:].bitcast(FP8X4), scales=par_scales[:], in_=par_grouped[:]
             )
 
-        pos_of, hit_of, off_of, squares_of, words_of, grouped_of, acc_of = {}, {}, {}, {}, {}, {}, {}
+        pos_of, which_of, hit_of, off_of, dist_of, squares_of = {}, {}, {}, {}, {}, {}
+        value_of, words_of, grouped_of, acc_of = {}, {}, {}, {}
 
         def rows_of(c):
             return min(CHUNK, ROWS - c * CHUNK)
@@ -129,22 +133,25 @@ def tile_bsplinekanlayer_s_kernel(tc, x, spline_parameters, w_b, w_s, out):
                 )
             pos_of[c] = pos
 
-        def nearest(c):
-            n = rows_of(c) * CAND
-            pos_v = pos_of[c][:].rearrange("p r c (q l) -> p (c q) r l", l=2)
-            which = work.tile([P, n], BF16)
+        def choose(c):
+            which = work.tile([P, rows_of(c) * CAND], BF16)
             nc.vector.tensor_scalar(
                 out=by_class(which[:]),
-                in0=pos_v,
+                in0=pos_of[c][:].rearrange("p r c (q l) -> p (c q) r l", l=2),
                 scalar1=ROUND_MAGIC,
                 scalar2=ROUND_MAGIC,
                 op0=ALU.add,
                 op1=ALU.subtract,
             )
+            which_of[c] = which
+
+        def offsets(c):
+            n = rows_of(c) * CAND
+            which = which_of[c]
             off = work.tile([P, n // 2], F32)
             nc.vector.tensor_tensor(
                 out=off[:].rearrange("p (a r l) -> p a r l", r=2, l=2),
-                in0=pos_v[:, :, 0:2, :],
+                in0=pos_of[c][:].rearrange("p r c (q l) -> p (c q) r l", l=2)[:, :, 0:2, :],
                 in1=by_class(which[:])[:, :, 0:2, :],
                 op=ALU.subtract,
             )
@@ -160,11 +167,14 @@ def tile_bsplinekanlayer_s_kernel(tc, x, spline_parameters, w_b, w_s, out):
             hit_of[c] = hit
             off_of[c] = off
 
+        def distance(c):
+            dist = work.tile([P, rows_of(c) * CAND // 2], F32)
+            nc.scalar.activation(out=dist[:], in_=off_of[c][:], func=ACT.Abs, scale=4.0)
+            dist_of[c] = dist
+
         def squares(c):
             n = rows_of(c) * CAND
-            dist = work.tile([P, n // 2], F32)
-            nc.scalar.activation(out=dist[:], in_=off_of[c][:], func=ACT.Abs, scale=4.0)
-            dist_v = dist[:].rearrange("p (a m) -> p a m", m=4)
+            dist_v = dist_of[c][:].rearrange("p (a m) -> p a m", m=4)
             wide = work.tile([P, n], F32)
             narrow = work.tile([P, n], F32)
             wide_v = wide[:].rearrange("p (a h m) -> p a h m", h=2, m=4)
@@ -179,14 +189,17 @@ def tile_bsplinekanlayer_s_kernel(tc, x, spline_parameters, w_b, w_s, out):
             nc.scalar.activation(out=narrow_sq[:], in_=narrow[:], func=ACT.Square, scale=math.sqrt(1.5))
             squares_of[c] = (wide_sq, narrow_sq)
 
-        def spread(c):
-            rows = rows_of(c)
-            n = rows * CAND
+        def round_value(c):
             wide_sq, narrow_sq = squares_of[c]
-            hit = hit_of[c]
-            value = work.tile([P, n], BF16)
+            value = work.tile([P, rows_of(c) * CAND], BF16)
             nc.vector.tensor_tensor(out=value[:], in0=wide_sq[:], in1=narrow_sq[:], op=ALU.subtract)
-            bases = work.tile([P, 4 * n], BF16)
+            value_of[c] = value
+
+        def place(c):
+            rows = rows_of(c)
+            hit = hit_of[c]
+            value = value_of[c]
+            bases = work.tile([P, 4 * rows * CAND], BF16)
             bases_w = bases[:].bitcast(F32)
             banks = []
             for g in range(rows // 2):
@@ -269,16 +282,20 @@ def tile_bsplinekanlayer_s_kernel(tc, x, spline_parameters, w_b, w_s, out):
                 stage(c)
 
         def step(t):
-            run(spread, t - 1)
-            run(squares, t)
+            run(round_value, t - 1)
+            run(choose, t + 1)
+            run(place, t - 1)
+            run(distance, t)
             run(positions, t + 2)
+            run(squares, t)
             run(regroup, t - 1)
-            run(nearest, t + 1)
+            run(offsets, t + 1)
             run(multiply, t - 2)
             run(finish, t - 3)
 
         transpose_parameters()
         step(-2)
+        regroup_parameters()
         step(-1)
         half_tanh()
         quantise_parameters()

@@ -1,5 +1,4 @@
 from contextlib import ExitStack
-import math
 
 import concourse.masks as masks
 import concourse.mybir as mybir
@@ -15,11 +14,10 @@ ALU = mybir.AluOpType
 P = 128
 BATCH, FEATURES, OUTS, BASES = 3584, 32, 128, 16
 ROWS = BATCH // P
-CHUNK = 6
-CHUNKS = -(-ROWS // CHUNK)
 PAIRS = FEATURES // 2
-RES = 4
-CAND = FEATURES * RES
+GROUPS = 4
+PARTS = (0, 4, 8, 12, 16, 20, 24, 26, 28)
+CHUNKS = ((0, 4), (4, 16), (16, 28))
 KNOTS_PER_UNIT = 57.0 / 7.0
 ROUND_MAGIC = 12582912.0
 
@@ -33,7 +31,9 @@ def tile_bsplinekanlayer_s_kernel(tc, x, spline_parameters, w_b, w_s, out):
 
     with ExitStack() as ctx:
         keep = ctx.enter_context(tc.tile_pool(name="keep", bufs=1))
+        evals = ctx.enter_context(tc.tile_pool(name="evals", bufs=3))
         work = ctx.enter_context(tc.tile_pool(name="work", bufs=3))
+        results = ctx.enter_context(tc.tile_pool(name="results", bufs=5))
         psum_words = ctx.enter_context(tc.psum_pool(name="psum_words", bufs=4))
         psum_acc = ctx.enter_context(tc.psum_pool(name="psum_acc", bufs=4))
         ctx.enter_context(tc.manual_schedule())
@@ -41,8 +41,9 @@ def tile_bsplinekanlayer_s_kernel(tc, x, spline_parameters, w_b, w_s, out):
         par_sb = keep.tile([P, FEATURES * BASES], BF16)
         nc.scalar.dma_start(out=par_sb[:], in_=spline_parameters.rearrange("o i k -> o (i k)"))
         x_sb = keep.tile([P, ROWS, FEATURES], BF16)
-        nc.sync.dma_start(out=x_sb[:, 0 : 2 * CHUNK, :], in_=x_rows[:, 0 : 2 * CHUNK, :])
-        nc.sync.dma_start(out=x_sb[:, 2 * CHUNK : ROWS, :], in_=x_rows[:, 2 * CHUNK : ROWS, :])
+        first = CHUNKS[1][1]
+        nc.sync.dma_start(out=x_sb[:, 0:first, :], in_=x_rows[:, 0:first, :])
+        nc.sync.dma_start(out=x_sb[:, first:ROWS, :], in_=x_rows[:, first:ROWS, :])
         wb_bf = keep.tile([P, 1], BF16)
         nc.sync.dma_start(out=wb_bf[:], in_=w_b.partition_broadcast(P))
         ws_bf = keep.tile([P, 1], BF16)
@@ -53,40 +54,37 @@ def tile_bsplinekanlayer_s_kernel(tc, x, spline_parameters, w_b, w_s, out):
 
         warm = keep.tile([P, 1], F32)
         nc.vector.memset(warm[:], 0.0)
-        nc.scalar.activation(out=warm[:], in_=warm[:], func=ACT.Abs)
+        nc.scalar.activation(out=warm[:], in_=warm[:], func=ACT.Silu)
 
         base_term = keep.tile([P, ROWS], F32)
         ws = keep.tile([P, 1], F32)
         par_codes = keep.tile([P, OUTS], U32, align_bytes=64)
         par_scales = keep.tile([P, OUTS], U8, align_bytes=64)
-        tanh = keep.tile([P, ROWS, FEATURES], F32)
+        silu = keep.tile([P, ROWS, FEATURES], F32)
         par_t = psum_words.tile([P, 2, OUTS], F32, tag="words")
 
-        def half_tanh():
-            nc.scalar.activation(out=tanh[:], in_=x_sb[:], func=ACT.Tanh, scale=0.5)
+        def silu_terms():
+            nc.scalar.activation(out=silu[:], in_=x_sb[:], func=ACT.Silu)
 
         def base_path():
-            twice_silu = keep.tile([P, ROWS, FEATURES], F32)
-            nc.vector.scalar_tensor_tensor(
-                out=twice_silu[:], in0=tanh[:], scalar=1.0, in1=x_sb[:], op0=ALU.add, op1=ALU.mult
-            )
             wb = keep.tile([P, 1], F32)
             nc.vector.tensor_copy(out=wb[:], in_=wb_bf[:])
             nc.vector.tensor_copy(out=ws[:], in_=ws_bf[:])
-            twice_sum = keep.tile([P, ROWS], F32)
-            nc.vector.tensor_reduce(
-                out=twice_sum[:], in_=twice_silu[:], axis=mybir.AxisListType.X, op=ALU.add
-            )
+            row_sum = keep.tile([P, ROWS], F32)
+            nc.vector.tensor_reduce(out=row_sum[:], in_=silu[:], axis=mybir.AxisListType.X, op=ALU.add)
             nc.vector.tensor_scalar(
-                out=base_term[:], in0=twice_sum[:], scalar1=wb[:, 0:1], scalar2=0.5, op0=ALU.mult, op1=ALU.mult
+                out=base_term[:], in0=row_sum[:], scalar1=wb[:, 0:1], scalar2=None, op0=ALU.mult
             )
 
         def transpose_parameters():
             par_pairs = keep.tile([P, 2 * P * 2], BF16)
-            par_src = par_sb[:].rearrange("o (q l u m) -> o u q m l", q=PAIRS, l=2, u=2, m=8)
-            par_dst = par_pairs[:].rearrange("o (u q m l) -> o u q m l", u=2, q=PAIRS, m=8, l=2)
+            par_src = par_sb[:].rearrange("o (q l u n d) -> o u d q n l", q=PAIRS, l=2, u=2, n=4, d=2)
+            par_dst = par_pairs[:].rearrange("o (u q n d l) -> o u d q n l", u=2, q=PAIRS, n=4, d=2, l=2)
             for u in range(2):
-                nc.vector.tensor_copy(out=par_dst[:, u], in_=par_src[:, u])
+                nc.vector.tensor_copy(out=par_dst[:, u, 0], in_=par_src[:, u, 0])
+                nc.vector.tensor_scalar(
+                    out=par_dst[:, u, 1], in0=par_src[:, u, 1], scalar1=-1.0, scalar2=None, op0=ALU.mult
+                )
             for u in range(2):
                 nc.tensor.transpose(
                     par_t[:, u, :], par_pairs[:].bitcast(F32)[:, u * P : (u + 1) * P], ident[:]
@@ -105,151 +103,154 @@ def tile_bsplinekanlayer_s_kernel(tc, x, spline_parameters, w_b, w_s, out):
                 out=par_codes[:].bitcast(FP8X4), scales=par_scales[:], in_=par_grouped[:]
             )
 
-        pos_of, which_of, hit_of, off_of, dist_of, squares_of = {}, {}, {}, {}, {}, {}
-        value_of, words_of, grouped_of, acc_of = {}, {}, {}, {}
+        pos_of, w_of, y_of, sign_of, dist_of = {}, {}, {}, {}, {}
+        square_of, wide_of, outer_of, value_of, hit_of = {}, {}, {}, {}, {}
 
-        def rows_of(c):
-            return min(CHUNK, ROWS - c * CHUNK)
+        def count_of(c):
+            return (CHUNKS[c][1] - CHUNKS[c][0]) * FEATURES
 
-        def by_class(flat):
-            return flat.rearrange("p (a r l) -> p a r l", r=RES, l=2)
+        def halves(planes):
+            return planes.rearrange("p h (a l) -> p a h l", l=2)
 
-        def by_pair(flat):
-            return flat.rearrange("p (c q m) -> p c q m", q=PAIRS, m=8)
-
-        def by_member(flat):
-            return flat.rearrange("p (c u q t m) -> p c u q t m", u=2, q=PAIRS, t=2, m=8)
+        def woven(flat):
+            return flat.rearrange("p (a h l) -> p a h l", h=2, l=2)
 
         def positions(c):
-            rows = rows_of(c)
-            pos = work.tile([P, RES, rows, FEATURES], F32)
-            for r in range(RES):
-                nc.scalar.activation(
-                    out=pos[:, r],
-                    in_=x_sb[:, c * CHUNK : c * CHUNK + rows, :],
-                    func=ACT.Identity,
-                    scale=KNOTS_PER_UNIT / 4.0,
-                    bias=(7.5 - r) / 4.0,
-                )
+            pos = evals.tile([P, count_of(c)], F32)
+            lo, hi = CHUNKS[c]
+            nc.scalar.activation(
+                out=pos[:].rearrange("p (t i) -> p t i", i=FEATURES),
+                in_=x_sb[:, lo:hi, :],
+                func=ACT.Identity,
+                scale=KNOTS_PER_UNIT / 4.0,
+                bias=9.0 / 4.0 - 0.5,
+            )
             pos_of[c] = pos
 
-        def choose(c):
-            which = work.tile([P, rows_of(c) * CAND], BF16)
+        def locate(c):
+            n = count_of(c)
+            w = evals.tile([P, 2, n], BF16)
             nc.vector.tensor_scalar(
-                out=by_class(which[:]),
-                in0=pos_of[c][:].rearrange("p r c (q l) -> p (c q) r l", l=2),
-                scalar1=ROUND_MAGIC,
-                scalar2=ROUND_MAGIC,
-                op0=ALU.add,
-                op1=ALU.subtract,
+                out=w[:, 0, :], in0=pos_of[c][:], scalar1=ROUND_MAGIC, scalar2=ROUND_MAGIC,
+                op0=ALU.add, op1=ALU.subtract,
             )
-            which_of[c] = which
+            y = evals.tile([P, n], F32)
+            nc.vector.tensor_tensor(out=y[:], in0=pos_of[c][:], in1=w[:, 0, :], op=ALU.subtract)
+            early = evals.tile([P, n], BF16)
+            nc.vector.tensor_scalar(out=early[:], in0=y[:], scalar1=0.0, scalar2=None, op0=ALU.is_lt)
+            nc.vector.tensor_tensor(out=w[:, 1, :], in0=w[:, 0, :], in1=early[:], op=ALU.subtract)
+            sign = evals.tile([P, 3, n], BF16)
+            nc.vector.tensor_scalar(
+                out=sign[:, 0:3:2, :], in0=early[:].unsqueeze(1).to_broadcast([P, 2, n]),
+                scalar1=0.5, scalar2=None, op0=ALU.subtract,
+            )
+            nc.vector.tensor_scalar(
+                out=sign[:, 1, :], in0=early[:], scalar1=-1.0, scalar2=0.5, op0=ALU.mult, op1=ALU.add
+            )
+            w_of[c], y_of[c], sign_of[c] = w, y, sign
 
-        def offsets(c):
-            n = rows_of(c) * CAND
-            which = which_of[c]
-            off = work.tile([P, n // 2], F32)
-            nc.vector.tensor_tensor(
-                out=off[:].rearrange("p (a r l) -> p a r l", r=2, l=2),
-                in0=pos_of[c][:].rearrange("p r c (q l) -> p (c q) r l", l=2)[:, :, 0:2, :],
-                in1=by_class(which[:])[:, :, 0:2, :],
-                op=ALU.subtract,
-            )
-            hit = work.tile([P, 4 * n], BF16)
-            for s in range(4):
+        def hits(c):
+            hit = evals.tile([P, GROUPS, 2 * count_of(c)], BF16)
+            for g in range(GROUPS):
                 nc.vector.tensor_scalar(
-                    out=by_member(hit[:])[:, :, s // 2, :, s % 2, :],
-                    in0=by_pair(which[:]),
-                    scalar1=float(s),
-                    scalar2=None,
+                    out=woven(hit[:, g, :]), in0=halves(w_of[c][:]), scalar1=float(g), scalar2=None,
                     op0=ALU.is_equal,
                 )
             hit_of[c] = hit
-            off_of[c] = off
-
-        def distance(c):
-            dist = work.tile([P, rows_of(c) * CAND // 2], F32)
-            nc.scalar.activation(out=dist[:], in_=off_of[c][:], func=ACT.Abs, scale=4.0)
-            dist_of[c] = dist
 
         def squares(c):
-            n = rows_of(c) * CAND
-            dist_v = dist_of[c][:].rearrange("p (a m) -> p a m", m=4)
-            wide = work.tile([P, n], F32)
-            narrow = work.tile([P, n], F32)
-            wide_v = wide[:].rearrange("p (a h m) -> p a h m", h=2, m=4)
-            narrow_v = narrow[:].rearrange("p (a h m) -> p a h m", h=2, m=4)
-            nc.scalar.activation(out=wide_v[:, :, 0, :], in_=dist_v, func=ACT.Relu, scale=-1.0, bias=1.5)
-            nc.scalar.activation(out=wide_v[:, :, 1, :], in_=dist_v, func=ACT.Relu, scale=1.0, bias=-0.5)
-            nc.scalar.activation(out=narrow_v[:, :, 0, :], in_=dist_v, func=ACT.Relu, scale=-1.0, bias=0.5)
-            nc.scalar.activation(out=narrow_v[:, :, 1, :], in_=dist_v, func=ACT.Relu, scale=1.0, bias=-1.5)
-            wide_sq = work.tile([P, n], F32)
-            nc.scalar.activation(out=wide_sq[:], in_=wide[:], func=ACT.Square, scale=math.sqrt(0.5))
-            narrow_sq = work.tile([P, n], F32)
-            nc.scalar.activation(out=narrow_sq[:], in_=narrow[:], func=ACT.Square, scale=math.sqrt(1.5))
-            squares_of[c] = (wide_sq, narrow_sq)
+            n = count_of(c)
+            dist = evals.tile([P, n], F32)
+            nc.scalar.activation(out=dist[:], in_=y_of[c][:], func=ACT.Abs, scale=4.0)
+            ramp = evals.tile([P, 2, n], F32)
+            nc.scalar.activation(out=ramp[:, 0, :], in_=dist[:], func=ACT.Relu, scale=-1.0, bias=1.0)
+            nc.scalar.activation(out=ramp[:, 1, :], in_=dist[:], func=ACT.Relu, scale=1.0, bias=-1.0)
+            wide = evals.tile([P, 2, n], F32)
+            nc.scalar.activation(out=wide[:, 0, :], in_=dist[:], func=ACT.Square, scale=-1.0, bias=2.0)
+            nc.scalar.activation(out=wide[:, 1, :], in_=dist[:], func=ACT.Square)
+            square = evals.tile([P, 2, n], F32)
+            nc.scalar.activation(out=square[:], in_=ramp[:], func=ACT.Square)
+            outer = evals.tile([P, 2, n], BF16)
+            nc.scalar.activation(out=outer[:], in_=ramp[:], func=ACT.Square)
+            square_of[c], wide_of[c], outer_of[c] = square, wide, outer
 
-        def round_value(c):
-            wide_sq, narrow_sq = squares_of[c]
-            value = work.tile([P, rows_of(c) * CAND], BF16)
-            nc.vector.tensor_tensor(out=value[:], in0=wide_sq[:], in1=narrow_sq[:], op=ALU.subtract)
+        def combine(c):
+            n = count_of(c)
+            inner = evals.tile([P, 2, n], BF16)
+            nc.vector.scalar_tensor_tensor(
+                out=inner[:], in0=square_of[c][:], scalar=-3.0, in1=wide_of[c][:], op0=ALU.mult, op1=ALU.add
+            )
+            outer_s = evals.tile([P, 2 * n], BF16)
+            nc.vector.tensor_tensor(
+                out=woven(outer_s[:]), in0=halves(outer_of[c][:]), in1=halves(sign_of[c][:, 1:3, :]), op=ALU.mult
+            )
+            inner_s = evals.tile([P, 2 * n], BF16)
+            nc.vector.tensor_tensor(
+                out=woven(inner_s[:]), in0=halves(inner[:]), in1=halves(sign_of[c][:, 0:2, :]), op=ALU.mult
+            )
+            value = evals.tile([P, 2, 2 * n], BF16)
+            nc.vector.tensor_tensor(out=value[:, 0, :], in0=inner_s[:], in1=outer_s[:], op=ALU.max)
+            nc.vector.tensor_tensor(out=value[:, 1, :], in0=inner_s[:], in1=outer_s[:], op=ALU.min)
             value_of[c] = value
 
-        def place(c):
-            rows = rows_of(c)
-            hit = hit_of[c]
-            value = value_of[c]
-            bases = work.tile([P, 4 * rows * CAND], BF16)
-            bases_w = bases[:].bitcast(F32)
-            banks = []
-            for g in range(rows // 2):
-                two = slice(2 * g, 2 * g + 2)
-                for u in range(2):
+        words_of, grouped_of, acc_of = {}, {}, {}
+
+        def rows_of(p):
+            return PARTS[p + 1] - PARTS[p]
+
+        def place(c, p):
+            rows = rows_of(p)
+            first = (PARTS[p] - CHUNKS[c][0]) * 2 * FEATURES
+            cols = slice(first, first + rows * 2 * FEATURES)
+            shape = [P, rows * PAIRS, 2, 2, 2]
+            bases = work.tile([P, 2, rows * 2 * P], BF16)
+            value = value_of[c][:, :, cols].rearrange("p e (a h l) -> p a h e l", h=2, l=2)
+            banks = [psum_words.tile([P, 2, 2 * P], F32, name="words") for g in range(rows // 2)]
+            for u in range(2):
+                by_group = bases[:, u, :].rearrange("p (a t h e l) -> p t a h e l", t=2, h=2, e=2, l=2)
+                for t in range(2):
                     nc.vector.tensor_tensor(
-                        out=by_member(bases[:])[:, two, u],
-                        in0=by_member(hit[:])[:, two, u],
-                        in1=by_pair(value[:])[:, two].unsqueeze(3).to_broadcast([P, 2, PAIRS, 2, 8]),
+                        out=by_group[:, t],
+                        in0=woven(hit_of[c][:, 2 * u + t, cols]).unsqueeze(3).to_broadcast(shape),
+                        in1=value,
                         op=ALU.mult,
                     )
-                words = psum_words.tile([P, 2, 2 * P], F32)
-                for h in range(2):
-                    for u in range(2):
-                        col = ((2 * g + h) * 2 + u) * P
-                        nc.tensor.transpose(
-                            words[:, u, h * P : (h + 1) * P], bases_w[:, col : col + P], ident[:]
-                        )
-                banks.append(words)
-            words_of[c] = banks
+                bases_w = bases[:, u, :].bitcast(F32)
+                for row in range(rows):
+                    nc.tensor.transpose(
+                        banks[row // 2][:, u, (row % 2) * P : (row % 2 + 1) * P],
+                        bases_w[:, row * P : (row + 1) * P],
+                        ident[:],
+                    )
+            words_of[p] = banks
 
-        def regroup(c):
-            rows = rows_of(c)
+        def regroup(p):
+            rows = rows_of(p)
             grouped = work.tile([P, rows * P * 4], BF16, align_bytes=64)
             grouped_v = grouped[:].bitcast(F32).rearrange("p (b u) -> p b u", u=2)
             for g in range(rows // 2):
                 nc.scalar.copy(
                     out=grouped_v[:, g * 2 * P : (g + 1) * 2 * P, :],
-                    in_=words_of[c][g][:].rearrange("p u b -> p b u"),
+                    in_=words_of[p][g][:].rearrange("p u b -> p b u"),
                 )
-            grouped_of[c] = grouped
+            grouped_of[p] = grouped
 
-        def multiply(c):
-            rows = rows_of(c)
+        def multiply(p):
+            rows = rows_of(p)
             codes = work.tile([P, rows * P], U32, align_bytes=64)
             scales = work.tile([P, rows * P], U8, align_bytes=64)
+            acc = psum_acc.tile([P, rows, OUTS], F32)
             for g in range(rows // 2):
                 cols = slice(g * 2 * P, (g + 1) * 2 * P)
                 nc.vector.quantize_mx(
                     out=codes[:, cols].bitcast(FP8X4),
                     scales=scales[:, cols],
-                    in_=grouped_of[c][:, g * 8 * P : (g + 1) * 8 * P],
+                    in_=grouped_of[p][:, g * 8 * P : (g + 1) * 8 * P],
                 )
-            accs = []
-            for first in range(0, rows, 4):
-                acc = psum_acc.tile([P, min(4, rows - first), OUTS], F32)
-                for row in range(first, min(first + 4, rows)):
+                for row in range(2 * g, 2 * g + 2):
                     cols = slice(row * P, (row + 1) * P)
                     nc.tensor.matmul_mx(
-                        out=acc[:, row - first, :],
+                        out=acc[:, row, :],
                         lhsT=codes[:, cols].bitcast(FP8X4),
                         lhsT_scale=scales[:, cols],
                         rhs=par_codes[:].bitcast(FP8X4),
@@ -257,49 +258,57 @@ def tile_bsplinekanlayer_s_kernel(tc, x, spline_parameters, w_b, w_s, out):
                         start=True,
                         stop=True,
                     )
-                accs.append(acc)
-            acc_of[c] = accs
+            acc_of[p] = acc
 
-        def finish(c):
-            rows = rows_of(c)
-            result = work.tile([P, rows, OUTS], F32)
-            for a, acc in enumerate(acc_of[c]):
-                k = acc.shape[1]
+        def finish(p, engine):
+            rows = rows_of(p)
+            result = results.tile([P, rows, OUTS], F32)
+            base = base_term[:, PARTS[p] : PARTS[p + 1]]
+            if engine == "vector":
                 nc.vector.scalar_tensor_tensor(
-                    out=result[:, 4 * a : 4 * a + k, :],
-                    in0=acc[:],
-                    scalar=ws[:, 0:1],
-                    in1=base_term[:, c * CHUNK + 4 * a : c * CHUNK + 4 * a + k]
-                    .unsqueeze(2)
-                    .to_broadcast([P, k, OUTS]),
-                    op0=ALU.mult,
-                    op1=ALU.add,
+                    out=result[:], in0=acc_of[p][:], scalar=ws[:, 0:1],
+                    in1=base.unsqueeze(2).to_broadcast([P, rows, OUTS]), op0=ALU.mult, op1=ALU.add,
                 )
-            nc.sync.dma_start(out=out_rows[:, c * CHUNK : c * CHUNK + rows, :], in_=result[:])
+            else:
+                for row in range(rows):
+                    nc.scalar.activation(
+                        out=result[:, row, :], in_=acc_of[p][:, row, :], func=ACT.Identity,
+                        scale=ws[:, 0:1], bias=base[:, row : row + 1],
+                    )
+            nc.sync.dma_start(out=out_rows[:, PARTS[p] : PARTS[p + 1], :], in_=result[:])
 
-        def run(stage, c):
-            if 0 <= c < CHUNKS:
-                stage(c)
-
-        def step(t):
-            run(round_value, t - 1)
-            run(choose, t + 1)
-            run(place, t - 1)
-            run(distance, t)
-            run(positions, t + 2)
-            run(squares, t)
-            run(regroup, t - 1)
-            run(offsets, t + 1)
-            run(multiply, t - 2)
-            run(finish, t - 3)
-
+        parts = len(PARTS) - 1
+        positions(0)
         transpose_parameters()
-        step(-2)
+        locate(0)
+        positions(1)
+        squares(0)
         regroup_parameters()
-        step(-1)
-        half_tanh()
+        hits(0)
+        locate(1)
         quantise_parameters()
-        step(0)
+        positions(2)
+        combine(0)
+        squares(1)
+        silu_terms()
+        place(0, 0)
+        regroup(0)
+        hits(1)
+        locate(2)
         base_path()
-        for t in range(1, CHUNKS + 3):
-            step(t)
+        squares(2)
+        chunk = 0
+        for p in range(1, parts + 3):
+            if p < parts:
+                if PARTS[p] == CHUNKS[chunk][1]:
+                    chunk += 1
+                    combine(chunk)
+                    if chunk == 1:
+                        hits(2)
+                place(chunk, p)
+            if 2 <= p < parts + 2:
+                multiply(p - 2)
+            if 3 <= p:
+                finish(p - 3, "vector" if p - 3 >= parts - 1 else "scalar")
+            if p < parts:
+                regroup(p)

@@ -80,15 +80,19 @@ def tile_bsplinekanlayer_s_kernel(tc, x, spline_parameters, w_b, w_s, out):
             par_pairs = keep.tile([P, 2 * P * 2], BF16)
             par_src = par_sb[:].rearrange("o (q l u n d) -> o u d q n l", q=PAIRS, l=2, u=2, n=4, d=2)
             par_dst = par_pairs[:].rearrange("o (u q n d l) -> o u d q n l", u=2, q=PAIRS, n=4, d=2, l=2)
-            for u in range(2):
+
+            def even(u):
                 nc.vector.tensor_copy(out=par_dst[:, u, 0], in_=par_src[:, u, 0])
+
+            def odd(u):
                 nc.vector.tensor_scalar(
                     out=par_dst[:, u, 1], in0=par_src[:, u, 1], scalar1=-1.0, scalar2=None, op0=ALU.mult
                 )
-            for u in range(2):
                 nc.tensor.transpose(
                     par_t[:, u, :], par_pairs[:].bitcast(F32)[:, u * P : (u + 1) * P], ident[:]
                 )
+
+            return [lambda: even(0), lambda: odd(0), lambda: even(1), lambda: odd(1)]
 
         par_grouped = keep.tile([P, OUTS * 4], BF16, align_bytes=64)
 
@@ -130,68 +134,92 @@ def tile_bsplinekanlayer_s_kernel(tc, x, spline_parameters, w_b, w_s, out):
         def locate(c):
             n = count_of(c)
             w = evals.tile([P, 2, n], BF16)
-            nc.vector.tensor_scalar(
-                out=w[:, 0, :], in0=pos_of[c][:], scalar1=ROUND_MAGIC, scalar2=ROUND_MAGIC,
-                op0=ALU.add, op1=ALU.subtract,
-            )
             y = evals.tile([P, n], F32)
-            nc.vector.tensor_tensor(out=y[:], in0=pos_of[c][:], in1=w[:, 0, :], op=ALU.subtract)
             early = evals.tile([P, n], BF16)
-            nc.vector.tensor_scalar(out=early[:], in0=y[:], scalar1=0.0, scalar2=None, op0=ALU.is_lt)
-            nc.vector.tensor_tensor(out=w[:, 1, :], in0=w[:, 0, :], in1=early[:], op=ALU.subtract)
-            sign = evals.tile([P, 3, n], BF16)
-            nc.vector.tensor_scalar(
-                out=sign[:, 0:3:2, :], in0=early[:].unsqueeze(1).to_broadcast([P, 2, n]),
-                scalar1=0.5, scalar2=None, op0=ALU.subtract,
-            )
-            nc.vector.tensor_scalar(
-                out=sign[:, 1, :], in0=early[:], scalar1=-1.0, scalar2=0.5, op0=ALU.mult, op1=ALU.add
-            )
+            sign = evals.tile([P, 2, n], BF16)
+            pos = pos_of[c]
             w_of[c], y_of[c], sign_of[c] = w, y, sign
+            return [
+                lambda: nc.vector.tensor_scalar(
+                    out=w[:, 0, :], in0=pos[:], scalar1=ROUND_MAGIC, scalar2=ROUND_MAGIC,
+                    op0=ALU.add, op1=ALU.subtract,
+                ),
+                lambda: nc.vector.tensor_tensor(out=y[:], in0=pos[:], in1=w[:, 0, :], op=ALU.subtract),
+                lambda: nc.vector.tensor_scalar(
+                    out=early[:], in0=y[:], scalar1=0.0, scalar2=None, op0=ALU.is_lt
+                ),
+                lambda: nc.vector.tensor_tensor(
+                    out=w[:, 1, :], in0=w[:, 0, :], in1=early[:], op=ALU.subtract
+                ),
+                lambda: nc.vector.tensor_scalar(
+                    out=sign[:, 1, :], in0=early[:], scalar1=0.5, scalar2=None, op0=ALU.subtract
+                ),
+                lambda: nc.vector.tensor_scalar(
+                    out=sign[:, 0, :], in0=early[:], scalar1=-1.0, scalar2=0.5, op0=ALU.mult, op1=ALU.add
+                ),
+            ]
 
         def hits(c):
             hit = evals.tile([P, GROUPS, 2 * count_of(c)], BF16)
-            for g in range(GROUPS):
+            hit_of[c] = hit
+
+            def one_group(g):
                 nc.vector.tensor_scalar(
                     out=woven(hit[:, g, :]), in0=halves(w_of[c][:]), scalar1=float(g), scalar2=None,
                     op0=ALU.is_equal,
                 )
-            hit_of[c] = hit
+
+            return [lambda g=g: one_group(g) for g in range(GROUPS)]
 
         def squares(c):
             n = count_of(c)
             dist = evals.tile([P, n], F32)
-            nc.scalar.activation(out=dist[:], in_=y_of[c][:], func=ACT.Abs, scale=4.0)
             ramp = evals.tile([P, 2, n], F32)
-            nc.scalar.activation(out=ramp[:, 0, :], in_=dist[:], func=ACT.Relu, scale=-1.0, bias=1.0)
-            nc.scalar.activation(out=ramp[:, 1, :], in_=dist[:], func=ACT.Relu, scale=1.0, bias=-1.0)
             wide = evals.tile([P, 2, n], F32)
-            nc.scalar.activation(out=wide[:, 0, :], in_=dist[:], func=ACT.Square, scale=-1.0, bias=2.0)
-            nc.scalar.activation(out=wide[:, 1, :], in_=dist[:], func=ACT.Square)
             square = evals.tile([P, 2, n], F32)
-            nc.scalar.activation(out=square[:], in_=ramp[:], func=ACT.Square)
             outer = evals.tile([P, 2, n], BF16)
-            nc.scalar.activation(out=outer[:], in_=ramp[:], func=ACT.Square)
             square_of[c], wide_of[c], outer_of[c] = square, wide, outer
+            y = y_of[c]
+
+            def act(out, in_, func, scale=1.0, bias=0.0):
+                return lambda: nc.scalar.activation(out=out, in_=in_, func=func, scale=scale, bias=bias)
+
+            return [
+                act(dist[:], y[:], ACT.Abs, scale=4.0),
+                act(ramp[:, 0, :], dist[:], ACT.Relu, scale=-1.0, bias=1.0),
+                act(ramp[:, 1, :], dist[:], ACT.Relu, scale=1.0, bias=-1.0),
+                act(wide[:, 0, :], dist[:], ACT.Square, scale=-1.0, bias=2.0),
+                act(wide[:, 1, :], dist[:], ACT.Square),
+                act(square[:], ramp[:], ACT.Square),
+                act(outer[:], ramp[:], ACT.Square),
+            ]
 
         def combine(c):
             n = count_of(c)
             inner = evals.tile([P, 2, n], BF16)
-            nc.vector.scalar_tensor_tensor(
-                out=inner[:], in0=square_of[c][:], scalar=-3.0, in1=wide_of[c][:], op0=ALU.mult, op1=ALU.add
-            )
             outer_s = evals.tile([P, 2 * n], BF16)
-            nc.vector.tensor_tensor(
-                out=woven(outer_s[:]), in0=halves(outer_of[c][:]), in1=halves(sign_of[c][:, 1:3, :]), op=ALU.mult
-            )
             inner_s = evals.tile([P, 2 * n], BF16)
-            nc.vector.tensor_tensor(
-                out=woven(inner_s[:]), in0=halves(inner[:]), in1=halves(sign_of[c][:, 0:2, :]), op=ALU.mult
-            )
             value = evals.tile([P, 2, 2 * n], BF16)
-            nc.vector.tensor_tensor(out=value[:, 0, :], in0=inner_s[:], in1=outer_s[:], op=ALU.max)
-            nc.vector.tensor_tensor(out=value[:, 1, :], in0=inner_s[:], in1=outer_s[:], op=ALU.min)
             value_of[c] = value
+            sign = halves(sign_of[c][:])
+            return [
+                lambda: nc.vector.scalar_tensor_tensor(
+                    out=inner[:], in0=square_of[c][:], scalar=3.0, in1=wide_of[c][:],
+                    op0=ALU.mult, op1=ALU.subtract,
+                ),
+                lambda: nc.vector.tensor_tensor(
+                    out=woven(outer_s[:]), in0=halves(outer_of[c][:]), in1=sign, op=ALU.mult
+                ),
+                lambda: nc.vector.tensor_tensor(
+                    out=woven(inner_s[:]), in0=halves(inner[:]), in1=sign, op=ALU.mult
+                ),
+                lambda: nc.vector.tensor_tensor(
+                    out=value[:, 0, :], in0=inner_s[:], in1=outer_s[:], op=ALU.max
+                ),
+                lambda: nc.vector.tensor_tensor(
+                    out=value[:, 1, :], in0=inner_s[:], in1=outer_s[:], op=ALU.min
+                ),
+            ]
 
         words_of, grouped_of, acc_of = {}, {}, {}
 
@@ -206,23 +234,24 @@ def tile_bsplinekanlayer_s_kernel(tc, x, spline_parameters, w_b, w_s, out):
             bases = work.tile([P, 2, rows * 2 * P], BF16)
             value = value_of[c][:, :, cols].rearrange("p e (a h l) -> p a h e l", h=2, l=2)
             banks = [psum_words.tile([P, 2, 2 * P], F32, name="words") for g in range(rows // 2)]
-            for u in range(2):
-                by_group = bases[:, u, :].rearrange("p (a t h e l) -> p t a h e l", t=2, h=2, e=2, l=2)
-                for t in range(2):
-                    nc.vector.tensor_tensor(
-                        out=by_group[:, t],
-                        in0=woven(hit_of[c][:, 2 * u + t, cols]).unsqueeze(3).to_broadcast(shape),
-                        in1=value,
-                        op=ALU.mult,
-                    )
-                bases_w = bases[:, u, :].bitcast(F32)
-                for row in range(rows):
-                    nc.tensor.transpose(
-                        banks[row // 2][:, u, (row % 2) * P : (row % 2 + 1) * P],
-                        bases_w[:, row * P : (row + 1) * P],
-                        ident[:],
-                    )
             words_of[p] = banks
+
+            def one_group(u, t):
+                nc.vector.tensor_tensor(
+                    out=bases[:, u, :].rearrange("p (a t h e l) -> p t a h e l", t=2, h=2, e=2, l=2)[:, t],
+                    in0=woven(hit_of[c][:, 2 * u + t, cols]).unsqueeze(3).to_broadcast(shape),
+                    in1=value,
+                    op=ALU.mult,
+                )
+                if t == 1:
+                    for row in range(rows):
+                        nc.tensor.transpose(
+                            banks[row // 2][:, u, (row % 2) * P : (row % 2 + 1) * P],
+                            bases[:, u, :].bitcast(F32)[:, row * P : (row + 1) * P],
+                            ident[:],
+                        )
+
+            return [lambda u=u, t=t: one_group(u, t) for u in range(2) for t in range(2)]
 
         def regroup(p):
             rows = rows_of(p)
@@ -277,35 +306,53 @@ def tile_bsplinekanlayer_s_kernel(tc, x, spline_parameters, w_b, w_s, out):
                     )
             nc.sync.dma_start(out=out_rows[:, PARTS[p] : PARTS[p + 1], :], in_=result[:])
 
+        def weave(first, second):
+            for i in range(max(len(first), len(second))):
+                for job in (first, second):
+                    if i < len(job):
+                        job[i]()
+
         parts = len(PARTS) - 1
         positions(0)
-        transpose_parameters()
-        locate(0)
         positions(1)
-        squares(0)
-        regroup_parameters()
-        hits(0)
-        locate(1)
-        quantise_parameters()
+        loc = locate(0)
+        sq = squares(0)
+        weave(transpose_parameters(), loc[0:2])
+        sq[0]()
+        loc[2]()
         positions(2)
-        combine(0)
-        squares(1)
+        loc1 = locate(1)
+        weave(loc[3:6], loc1[0:2])
+        sq1 = squares(1)
+        for job in sq[1:7]:
+            job()
+        loc1[2]()
+        weave(hits(0), [regroup_parameters] + loc1[3:6])
+        sq1[0]()
         silu_terms()
-        place(0, 0)
+        quantise_parameters()
+        comb = combine(0)
+        hit1 = hits(1)
+        for job in sq1[1:7]:
+            job()
+        weave(comb[0:2], hit1[0:1])
+        weave(comb[2:4], hit1[1:2])
+        comb[4]()
+        loc2 = locate(2)
+        weave(place(0, 0), hit1[2:4] + loc2[0:2])
+        sq2 = squares(2)
         regroup(0)
-        hits(1)
-        locate(2)
         base_path()
-        squares(2)
-        chunk = 0
+        comb = combine(1)
+        weave(comb[0:2], loc2[2:3])
+        weave(comb[2:5], loc2[3:6])
+        for job in sq2:
+            job()
+        extra = {1: hits(2), 3: combine(2)}
         for p in range(1, parts + 3):
+            chunk = 1 if p < 4 else 2
             if p < parts:
-                if PARTS[p] == CHUNKS[chunk][1]:
-                    chunk += 1
-                    combine(chunk)
-                    if chunk == 1:
-                        hits(2)
-                place(chunk, p)
+                weave(place(chunk, p), extra.get(p, []))
             if 2 <= p < parts + 2:
                 multiply(p - 2)
             if 3 <= p:

@@ -15,8 +15,9 @@ P = 128
 BATCH, FEATURES, OUTS, BASES = 3584, 32, 128, 16
 ROWS = BATCH // P
 PAIRS = FEATURES // 2
+SHARE = P // FEATURES
 GROUPS = 4
-PARTS = (0, 4, 8, 12, 16, 20, 24, 26, 28)
+PARTS = (0, 4, 8, 12, 16, 20, 24, 28)
 CHUNKS = ((0, 4), (4, 16), (16, 28))
 KNOTS_PER_UNIT = 57.0 / 7.0
 ROUND_MAGIC = 12582912.0
@@ -60,26 +61,49 @@ def tile_bsplinekanlayer_s_kernel(tc, x, spline_parameters, w_b, w_s, out):
         ws = keep.tile([P, 1], F32)
         par_codes = keep.tile([P, OUTS], U32, align_bytes=64)
         par_scales = keep.tile([P, OUTS], U8, align_bytes=64)
-        silu = keep.tile([P, ROWS, FEATURES], F32)
         par_t = psum_words.tile([P, 2, OUTS], F32, tag="words")
+        wb = keep.tile([P, 1], F32)
+        row_of = keep.tile([P, SHARE], F32)
+        ident_bf = keep.tile([P, P], BF16)
+        x_t = psum_words.tile([P, ROWS // SHARE, P], BF16, tag="words")
+        silu = keep.tile([P, ROWS // SHARE, P], F32)
+        row_sum = psum_words.tile([P, ROWS], F32, tag="words")
+
+        def constants():
+            masks.make_identity(nc, ident_bf[:])
+            nc.gpsimd.memset(row_of[:], 0.0)
+            for r in range(SHARE):
+                nc.gpsimd.memset(row_of[r * FEATURES : (r + 1) * FEATURES, r : r + 1], 1.0)
+
+        def transpose_x():
+            for g in range(ROWS // SHARE):
+                nc.tensor.transpose(
+                    x_t[:, g, :], x_sb[:, g * SHARE : (g + 1) * SHARE, :].rearrange("p t i -> p (t i)"), ident_bf[:]
+                )
 
         def silu_terms():
-            nc.scalar.activation(out=silu[:], in_=x_sb[:], func=ACT.Silu)
+            nc.scalar.activation(out=silu[:], in_=x_t[:], func=ACT.Silu)
 
-        def base_path():
-            wb = keep.tile([P, 1], F32)
+        def sum_silu():
+            for g in range(ROWS // SHARE):
+                nc.tensor.matmul(
+                    out=row_sum[:, g * SHARE : (g + 1) * SHARE], lhsT=silu[:, g, :], rhs=row_of[:],
+                    start=True, stop=True,
+                )
+
+        def widen_gains():
             nc.vector.tensor_copy(out=wb[:], in_=wb_bf[:])
             nc.vector.tensor_copy(out=ws[:], in_=ws_bf[:])
-            row_sum = keep.tile([P, ROWS], F32)
-            nc.vector.tensor_reduce(out=row_sum[:], in_=silu[:], axis=mybir.AxisListType.X, op=ALU.add)
+
+        def base_path():
             nc.vector.tensor_scalar(
                 out=base_term[:], in0=row_sum[:], scalar1=wb[:, 0:1], scalar2=None, op0=ALU.mult
             )
 
         def transpose_parameters():
             par_pairs = keep.tile([P, 2 * P * 2], BF16)
-            par_src = par_sb[:].rearrange("o (q l u n d) -> o u d q n l", q=PAIRS, l=2, u=2, n=4, d=2)
-            par_dst = par_pairs[:].rearrange("o (u q n d l) -> o u d q n l", u=2, q=PAIRS, n=4, d=2, l=2)
+            par_src = par_sb[:].rearrange("o (q l u t h e) -> o u e q t h l", q=PAIRS, l=2, u=2, t=2, h=2)
+            par_dst = par_pairs[:].rearrange("o (u q t e h l) -> o u e q t h l", u=2, q=PAIRS, t=2, e=2, h=2)
 
             def even(u):
                 nc.vector.tensor_copy(out=par_dst[:, u, 0], in_=par_src[:, u, 0])
@@ -232,14 +256,14 @@ def tile_bsplinekanlayer_s_kernel(tc, x, spline_parameters, w_b, w_s, out):
             cols = slice(first, first + rows * 2 * FEATURES)
             shape = [P, rows * PAIRS, 2, 2, 2]
             bases = work.tile([P, 2, rows * 2 * P], BF16)
-            value = value_of[c][:, :, cols].rearrange("p e (a h l) -> p a h e l", h=2, l=2)
+            value = value_of[c][:, :, cols].rearrange("p e (a h l) -> p a e h l", h=2, l=2)
             banks = [psum_words.tile([P, 2, 2 * P], F32, name="words") for g in range(rows // 2)]
             words_of[p] = banks
 
             def one_group(u, t):
                 nc.vector.tensor_tensor(
-                    out=bases[:, u, :].rearrange("p (a t h e l) -> p t a h e l", t=2, h=2, e=2, l=2)[:, t],
-                    in0=woven(hit_of[c][:, 2 * u + t, cols]).unsqueeze(3).to_broadcast(shape),
+                    out=bases[:, u, :].rearrange("p (a t e h l) -> p t a e h l", t=2, e=2, h=2, l=2)[:, t],
+                    in0=woven(hit_of[c][:, 2 * u + t, cols]).unsqueeze(2).to_broadcast(shape),
                     in1=value,
                     op=ALU.mult,
                 )
@@ -306,56 +330,63 @@ def tile_bsplinekanlayer_s_kernel(tc, x, spline_parameters, w_b, w_s, out):
                     )
             nc.sync.dma_start(out=out_rows[:, PARTS[p] : PARTS[p + 1], :], in_=result[:])
 
+        def run(jobs):
+            for job in jobs:
+                job()
+
         def weave(first, second):
             for i in range(max(len(first), len(second))):
-                for job in (first, second):
-                    if i < len(job):
-                        job[i]()
+                run(first[i : i + 1])
+                run(second[i : i + 1])
 
         parts = len(PARTS) - 1
+        constants()
         positions(0)
         positions(1)
+        transpose_x()
+        par = transpose_parameters()
         loc = locate(0)
-        sq = squares(0)
-        weave(transpose_parameters(), loc[0:2])
-        sq[0]()
-        loc[2]()
-        positions(2)
         loc1 = locate(1)
-        weave(loc[3:6], loc1[0:2])
+        sq = squares(0)
+        weave(par[0:2], loc[0:2])
+        run(sq[0:1])
+        positions(2)
+        weave(loc1[0:1] + par[2:4] + loc1[1:2], loc[2:6])
+        run(sq[1:7])
+        hit = hits(0)
+        weave(loc1[2:4], hit[0:2])
         sq1 = squares(1)
-        for job in sq[1:7]:
-            job()
-        loc1[2]()
-        weave(hits(0), [regroup_parameters] + loc1[3:6])
-        sq1[0]()
+        run(sq1[0:1])
         silu_terms()
-        quantise_parameters()
-        comb = combine(0)
+        run(sq1[1:7])
+        sum_silu()
+        weave(loc1[4:6], hit[2:4])
         hit1 = hits(1)
-        for job in sq1[1:7]:
-            job()
-        weave(comb[0:2], hit1[0:1])
-        weave(comb[2:4], hit1[1:2])
-        comb[4]()
+        comb = combine(0)
+        regroup_parameters()
+        run(hit1[0:1])
+        weave(comb[0:2], hit1[1:2])
+        quantise_parameters()
+        weave(comb[2:4], hit1[2:3])
+        run(comb[4:5])
+        run(hit1[3:4])
         loc2 = locate(2)
-        weave(place(0, 0), hit1[2:4] + loc2[0:2])
+        weave(place(0, 0), loc2[0:3])
+        widen_gains()
         sq2 = squares(2)
         regroup(0)
-        base_path()
         comb = combine(1)
-        weave(comb[0:2], loc2[2:3])
-        weave(comb[2:5], loc2[3:6])
-        for job in sq2:
-            job()
+        weave(comb[0:2], loc2[3:4])
+        weave(comb[2:5], loc2[4:6])
+        base_path()
+        run(sq2)
         extra = {1: hits(2), 3: combine(2)}
-        for p in range(1, parts + 3):
-            chunk = 1 if p < 4 else 2
+        for p in range(1, parts + 4):
+            chunk = 1 if PARTS[min(p, parts)] < CHUNKS[1][1] else 2
             if p < parts:
                 weave(place(chunk, p), extra.get(p, []))
-            if 2 <= p < parts + 2:
-                multiply(p - 2)
-            if 3 <= p:
-                finish(p - 3, "vector" if p - 3 >= parts - 1 else "scalar")
-            if p < parts:
                 regroup(p)
+            if 3 <= p < parts + 3:
+                multiply(p - 3)
+            if 4 <= p:
+                finish(p - 4, "vector" if p - 4 >= parts - 2 else "scalar")

@@ -17,7 +17,7 @@ ROWS = BATCH // P
 PAIRS = FEATURES // 2
 SHARE = P // FEATURES
 GROUPS = 4
-PARTS = (0, 4, 8, 12, 16, 20, 24, 28)
+PARTS = (0, 4, 8, 12, 16, 20, 24, 26, 28)
 CHUNKS = ((0, 4), (4, 16), (16, 28))
 KNOTS_PER_UNIT = 57.0 / 7.0
 ROUND_MAGIC = 12582912.0
@@ -33,7 +33,7 @@ def tile_bsplinekanlayer_s_kernel(tc, x, spline_parameters, w_b, w_s, out):
     with ExitStack() as ctx:
         keep = ctx.enter_context(tc.tile_pool(name="keep", bufs=1))
         evals = ctx.enter_context(tc.tile_pool(name="evals", bufs=3))
-        work = ctx.enter_context(tc.tile_pool(name="work", bufs=3))
+        work = ctx.enter_context(tc.tile_pool(name="work", bufs=4))
         results = ctx.enter_context(tc.tile_pool(name="results", bufs=5))
         psum_words = ctx.enter_context(tc.psum_pool(name="psum_words", bufs=4))
         psum_acc = ctx.enter_context(tc.psum_pool(name="psum_acc", bufs=4))
@@ -144,42 +144,42 @@ def tile_bsplinekanlayer_s_kernel(tc, x, spline_parameters, w_b, w_s, out):
             return flat.rearrange("p (a h l) -> p a h l", h=2, l=2)
 
         def positions(c):
-            pos = evals.tile([P, count_of(c)], F32)
-            lo, hi = CHUNKS[c]
-            nc.scalar.activation(
-                out=pos[:].rearrange("p (t i) -> p t i", i=FEATURES),
-                in_=x_sb[:, lo:hi, :],
-                func=ACT.Identity,
-                scale=KNOTS_PER_UNIT / 4.0,
-                bias=9.0 / 4.0 - 0.5,
-            )
+            pos = evals.tile([P, 2, count_of(c)], F32)
             pos_of[c] = pos
+            lo, hi = CHUNKS[c]
+
+            def one_half(h):
+                out = pos[:, h, :].rearrange("p (t i) -> p t i", i=FEATURES)
+                scale, bias = KNOTS_PER_UNIT / 4.0, 9.0 / 4.0 - (h + 1) / 2.0
+                if c == 0:
+                    nc.vector.tensor_scalar(
+                        out=out, in0=x_sb[:, lo:hi, :], scalar1=scale, scalar2=bias, op0=ALU.mult, op1=ALU.add
+                    )
+                else:
+                    nc.scalar.activation(
+                        out=out, in_=x_sb[:, lo:hi, :], func=ACT.Identity, scale=scale, bias=bias
+                    )
+
+            return [lambda: one_half(0), lambda: one_half(1)]
 
         def locate(c):
             n = count_of(c)
             w = evals.tile([P, 2, n], BF16)
             y = evals.tile([P, n], F32)
-            early = evals.tile([P, n], BF16)
             sign = evals.tile([P, 2, n], BF16)
             pos = pos_of[c]
             w_of[c], y_of[c], sign_of[c] = w, y, sign
             return [
                 lambda: nc.vector.tensor_scalar(
-                    out=w[:, 0, :], in0=pos[:], scalar1=ROUND_MAGIC, scalar2=ROUND_MAGIC,
+                    out=w[:], in0=pos[:], scalar1=ROUND_MAGIC, scalar2=ROUND_MAGIC,
                     op0=ALU.add, op1=ALU.subtract,
                 ),
-                lambda: nc.vector.tensor_tensor(out=y[:], in0=pos[:], in1=w[:, 0, :], op=ALU.subtract),
+                lambda: nc.vector.tensor_tensor(out=y[:], in0=pos[:, 0, :], in1=w[:, 0, :], op=ALU.subtract),
                 lambda: nc.vector.tensor_scalar(
-                    out=early[:], in0=y[:], scalar1=0.0, scalar2=None, op0=ALU.is_lt
-                ),
-                lambda: nc.vector.tensor_tensor(
-                    out=w[:, 1, :], in0=w[:, 0, :], in1=early[:], op=ALU.subtract
+                    out=sign[:, 1, :], in0=y[:], scalar1=0.0, scalar2=0.5, op0=ALU.is_lt, op1=ALU.subtract
                 ),
                 lambda: nc.vector.tensor_scalar(
-                    out=sign[:, 1, :], in0=early[:], scalar1=0.5, scalar2=None, op0=ALU.subtract
-                ),
-                lambda: nc.vector.tensor_scalar(
-                    out=sign[:, 0, :], in0=early[:], scalar1=-1.0, scalar2=0.5, op0=ALU.mult, op1=ALU.add
+                    out=sign[:, 0, :], in0=sign[:, 1, :], scalar1=-1.0, scalar2=None, op0=ALU.mult
                 ),
             ]
 
@@ -341,52 +341,64 @@ def tile_bsplinekanlayer_s_kernel(tc, x, spline_parameters, w_b, w_s, out):
 
         parts = len(PARTS) - 1
         constants()
-        positions(0)
-        positions(1)
-        transpose_x()
+        pos, pos1, pos2 = positions(0), positions(1), positions(2)
         par = transpose_parameters()
-        loc = locate(0)
-        loc1 = locate(1)
-        sq = squares(0)
-        weave(par[0:2], loc[0:2])
+        loc, loc1, loc2 = locate(0), locate(1), locate(2)
+        sq, sq1, sq2 = squares(0), squares(1), squares(2)
+        hit, hit1, hit2 = hits(0), hits(1), hits(2)
+        comb, comb1, comb2 = combine(0), combine(1), combine(2)
+        run(pos1)
+        run(pos)
+        transpose_x()
+        run(par[0:2])
+        run(loc[0:1])
+        run(par[2:4])
+        run(loc[1:2])
         run(sq[0:1])
-        positions(2)
-        weave(loc1[0:1] + par[2:4] + loc1[1:2], loc[2:6])
+        run(loc1[0:1])
+        weave(loc[2:4], hit[0:2])
+        run(hit[2:4])
+        run(loc1[1:2])
+        run(pos2[0:1])
         run(sq[1:7])
-        hit = hits(0)
-        weave(loc1[2:4], hit[0:2])
-        sq1 = squares(1)
-        run(sq1[0:1])
-        silu_terms()
-        run(sq1[1:7])
-        sum_silu()
-        weave(loc1[4:6], hit[2:4])
-        hit1 = hits(1)
-        comb = combine(0)
         regroup_parameters()
+        run(loc1[2:3])
         run(hit1[0:1])
-        weave(comb[0:2], hit1[1:2])
+        run(loc1[3:4])
+        run(sq1[0:1])
+        run(pos2[1:2])
+        run(sq1[1:7])
         quantise_parameters()
+        weave(comb[0:2], hit1[1:2])
         weave(comb[2:4], hit1[2:3])
         run(comb[4:5])
         run(hit1[3:4])
-        loc2 = locate(2)
         weave(place(0, 0), loc2[0:3])
-        widen_gains()
-        sq2 = squares(2)
+        silu_terms()
         regroup(0)
-        comb = combine(1)
-        weave(comb[0:2], loc2[3:4])
-        weave(comb[2:5], loc2[4:6])
-        base_path()
         run(sq2)
-        extra = {1: hits(2), 3: combine(2)}
-        for p in range(1, parts + 4):
-            chunk = 1 if PARTS[min(p, parts)] < CHUNKS[1][1] else 2
-            if p < parts:
-                weave(place(chunk, p), extra.get(p, []))
-                regroup(p)
-            if 3 <= p < parts + 3:
-                multiply(p - 3)
-            if 4 <= p:
-                finish(p - 4, "vector" if p - 4 >= parts - 2 else "scalar")
+        sum_silu()
+        widen_gains()
+        run(loc2[3:4])
+        run(hit2[0:1])
+        run(comb1[0:3])
+        run(hit2[1:2])
+        run(comb1[3:5])
+        run(hit2[2:3])
+        extra = {1: hit2[3:4], 2: [base_path] + comb2[0:1], 3: comb2[1:5]}
+        chunk = 0
+        for p in range(1, parts):
+            if PARTS[p] == CHUNKS[chunk][1]:
+                chunk += 1
+            weave(place(chunk, p), extra.get(p, []))
+            regroup(p)
+            if p >= 2:
+                multiply(p - 2)
+            if 2 <= p < parts - 2:
+                finish(p - 2, "scalar")
+        finish(parts - 4, "vector")
+        finish(parts - 3, "scalar")
+        multiply(parts - 2)
+        finish(parts - 2, "scalar")
+        multiply(parts - 1)
+        finish(parts - 1, "vector")

@@ -33,7 +33,7 @@ def tile_bsplinekanlayer_s_kernel(tc, x, spline_parameters, w_b, w_s, out):
     with ExitStack() as ctx:
         keep = ctx.enter_context(tc.tile_pool(name="keep", bufs=1))
         evals = ctx.enter_context(tc.tile_pool(name="evals", bufs=3))
-        work = ctx.enter_context(tc.tile_pool(name="work", bufs=4))
+        work = ctx.enter_context(tc.tile_pool(name="work", bufs=5))
         results = ctx.enter_context(tc.tile_pool(name="results", bufs=5))
         psum_words = ctx.enter_context(tc.psum_pool(name="psum_words", bufs=4))
         psum_acc = ctx.enter_context(tc.psum_pool(name="psum_acc", bufs=4))
@@ -132,7 +132,7 @@ def tile_bsplinekanlayer_s_kernel(tc, x, spline_parameters, w_b, w_s, out):
             )
 
         pos_of, w_of, y_of, sign_of, dist_of = {}, {}, {}, {}, {}
-        square_of, wide_of, outer_of, value_of, hit_of = {}, {}, {}, {}, {}
+        inner_of, edge_of, outer_of, value_of, hit_of = {}, {}, {}, {}, {}
 
         def count_of(c):
             return (CHUNKS[c][1] - CHUNKS[c][0]) * FEATURES
@@ -199,10 +199,11 @@ def tile_bsplinekanlayer_s_kernel(tc, x, spline_parameters, w_b, w_s, out):
             n = count_of(c)
             dist = evals.tile([P, n], F32)
             ramp = evals.tile([P, 2, n], F32)
-            wide = evals.tile([P, 2, n], F32)
-            square = evals.tile([P, 2, n], F32)
+            bump = evals.tile([P, 2, n], F32)
+            inner = evals.tile([P, 2, n], BF16)
             outer = evals.tile([P, 2, n], BF16)
-            square_of[c], wide_of[c], outer_of[c] = square, wide, outer
+            edge = evals.tile([P, 2, n], BF16)
+            inner_of[c], edge_of[c], outer_of[c] = inner, edge, outer
             y = y_of[c]
 
             def act(out, in_, func, scale=1.0, bias=0.0):
@@ -212,30 +213,28 @@ def tile_bsplinekanlayer_s_kernel(tc, x, spline_parameters, w_b, w_s, out):
                 act(dist[:], y[:], ACT.Abs, scale=4.0),
                 act(ramp[:, 0, :], dist[:], ACT.Relu, scale=-1.0, bias=1.0),
                 act(ramp[:, 1, :], dist[:], ACT.Relu, scale=1.0, bias=-1.0),
-                act(wide[:, 0, :], dist[:], ACT.Square, scale=-1.0, bias=2.0),
-                act(wide[:, 1, :], dist[:], ACT.Square),
-                act(square[:], ramp[:], ACT.Square),
+                act(edge[:, 1, :], ramp[:, 0, :], ACT.Square, scale=-1.0, bias=1.0),
+                act(edge[:, 0, :], ramp[:, 1, :], ACT.Square, scale=-1.0, bias=1.0),
+                act(bump[:], ramp[:], ACT.Square, bias=-0.5),
                 act(outer[:], ramp[:], ACT.Square),
+                act(inner[:], bump[:], ACT.Identity, scale=2.0, bias=-1.5),
             ]
 
         def combine(c):
             n = count_of(c)
-            inner = evals.tile([P, 2, n], BF16)
+            edge_s = evals.tile([P, 2, n], BF16)
             outer_s = evals.tile([P, 2 * n], BF16)
             inner_s = evals.tile([P, 2 * n], BF16)
             value = evals.tile([P, 2, 2 * n], BF16)
             value_of[c] = value
-            sign = halves(sign_of[c][:])
+            sign = sign_of[c]
             return [
-                lambda: nc.vector.scalar_tensor_tensor(
-                    out=inner[:], in0=square_of[c][:], scalar=3.0, in1=wide_of[c][:],
-                    op0=ALU.mult, op1=ALU.subtract,
+                lambda: nc.vector.tensor_tensor(out=edge_s[:], in0=edge_of[c][:], in1=sign[:], op=ALU.mult),
+                lambda: nc.vector.tensor_tensor(
+                    out=woven(outer_s[:]), in0=halves(outer_of[c][:]), in1=halves(sign[:]), op=ALU.mult
                 ),
                 lambda: nc.vector.tensor_tensor(
-                    out=woven(outer_s[:]), in0=halves(outer_of[c][:]), in1=sign, op=ALU.mult
-                ),
-                lambda: nc.vector.tensor_tensor(
-                    out=woven(inner_s[:]), in0=halves(inner[:]), in1=sign, op=ALU.mult
+                    out=woven(inner_s[:]), in0=halves(inner_of[c][:]), in1=halves(edge_s[:]), op=ALU.mult
                 ),
                 lambda: nc.vector.tensor_tensor(
                     out=value[:, 0, :], in0=inner_s[:], in1=outer_s[:], op=ALU.max
@@ -360,14 +359,14 @@ def tile_bsplinekanlayer_s_kernel(tc, x, spline_parameters, w_b, w_s, out):
         run(hit[2:4])
         run(loc1[1:2])
         run(pos2[0:1])
-        run(sq[1:7])
+        run(sq[1:8])
         regroup_parameters()
         run(loc1[2:3])
         run(hit1[0:1])
         run(loc1[3:4])
         run(sq1[0:1])
         run(pos2[1:2])
-        run(sq1[1:7])
+        run(sq1[1:8])
         quantise_parameters()
         weave(comb[0:2], hit1[1:2])
         weave(comb[2:4], hit1[2:3])
@@ -392,13 +391,15 @@ def tile_bsplinekanlayer_s_kernel(tc, x, spline_parameters, w_b, w_s, out):
                 chunk += 1
             weave(place(chunk, p), extra.get(p, []))
             regroup(p)
-            if p >= 2:
+            if 2 <= p < parts - 3:
                 multiply(p - 2)
-            if 2 <= p < parts - 2:
                 finish(p - 2, "scalar")
-        finish(parts - 4, "vector")
-        finish(parts - 3, "scalar")
+        for p in range(parts - 5, parts - 2):
+            multiply(p)
+        finish(parts - 5, "vector")
+        finish(parts - 4, "scalar")
         multiply(parts - 2)
-        finish(parts - 2, "scalar")
+        finish(parts - 3, "scalar")
         multiply(parts - 1)
+        finish(parts - 2, "scalar")
         finish(parts - 1, "vector")

@@ -84,8 +84,8 @@ def tile_bsplinekanlayer_s_kernel(tc, x, spline_parameters, w_b, w_s, out):
         def silu_terms():
             nc.scalar.activation(out=silu[:], in_=x_t[:], func=ACT.Silu)
 
-        def sum_silu():
-            for g in range(ROWS // SHARE):
+        def sum_silu(shares):
+            for g in shares:
                 nc.tensor.matmul(
                     out=row_sum[:, g * SHARE : (g + 1) * SHARE], lhsT=silu[:, g, :], rhs=row_of[:],
                     start=True, stop=True,
@@ -102,21 +102,22 @@ def tile_bsplinekanlayer_s_kernel(tc, x, spline_parameters, w_b, w_s, out):
 
         def transpose_parameters():
             par_pairs = keep.tile([P, 2 * P * 2], BF16)
-            par_src = par_sb[:].rearrange("o (q l u t h e) -> o u e q t h l", q=PAIRS, l=2, u=2, t=2, h=2)
-            par_dst = par_pairs[:].rearrange("o (u q t e h l) -> o u e q t h l", u=2, q=PAIRS, t=2, e=2, h=2)
+            par_src = par_sb[:].rearrange("o (q l u t v) -> o u q t v l", q=PAIRS, l=2, u=2, t=2, v=4)
+            par_dst = par_pairs[:].rearrange("o (u q t d h l) -> o u d q t h l", u=2, q=PAIRS, t=2, d=2, h=2)
 
-            def even(u):
-                nc.vector.tensor_copy(out=par_dst[:, u, 0], in_=par_src[:, u, 0])
+            def pick(u, d):
+                picked = par_src[:, u, :, :, 1:3, :] if d == 0 else par_src[:, u, :, :, 0:4:3, :]
+                nc.vector.tensor_copy(out=par_dst[:, u, d], in_=picked)
 
-            def odd(u):
-                nc.vector.tensor_scalar(
-                    out=par_dst[:, u, 1], in0=par_src[:, u, 1], scalar1=-1.0, scalar2=None, op0=ALU.mult
-                )
-                nc.tensor.transpose(
-                    par_t[:, u, :], par_pairs[:].bitcast(F32)[:, u * P : (u + 1) * P], ident[:]
-                )
+            def negate():
+                smaller = par_pairs[:].rearrange("o (a d m) -> o a d m", d=2, m=4)[:, :, 1, :]
+                nc.vector.tensor_scalar(out=smaller, in0=smaller, scalar1=-1.0, scalar2=None, op0=ALU.mult)
+                for u in range(2):
+                    nc.tensor.transpose(
+                        par_t[:, u, :], par_pairs[:].bitcast(F32)[:, u * P : (u + 1) * P], ident[:]
+                    )
 
-            return [lambda: even(0), lambda: odd(0), lambda: even(1), lambda: odd(1)]
+            return [lambda u=u, d=d: pick(u, d) for u in range(2) for d in range(2)] + [negate]
 
         par_grouped = keep.tile([P, OUTS * 4], BF16, align_bytes=64)
 
@@ -151,7 +152,7 @@ def tile_bsplinekanlayer_s_kernel(tc, x, spline_parameters, w_b, w_s, out):
             def one_half(h):
                 out = pos[:, h, :].rearrange("p (t i) -> p t i", i=FEATURES)
                 scale, bias = KNOTS_PER_UNIT / 4.0, 9.0 / 4.0 - (h + 1) / 2.0
-                if c == 0:
+                if c != 1:
                     nc.vector.tensor_scalar(
                         out=out, in0=x_sb[:, lo:hi, :], scalar1=scale, scalar2=bias, op0=ALU.mult, op1=ALU.add
                     )
@@ -166,7 +167,7 @@ def tile_bsplinekanlayer_s_kernel(tc, x, spline_parameters, w_b, w_s, out):
             n = count_of(c)
             w = evals.tile([P, 2, n], BF16)
             y = evals.tile([P, n], F32)
-            sign = evals.tile([P, 2, n], BF16)
+            sign = evals.tile([P, n], BF16)
             pos = pos_of[c]
             w_of[c], y_of[c], sign_of[c] = w, y, sign
             return [
@@ -176,10 +177,7 @@ def tile_bsplinekanlayer_s_kernel(tc, x, spline_parameters, w_b, w_s, out):
                 ),
                 lambda: nc.vector.tensor_tensor(out=y[:], in0=pos[:, 0, :], in1=w[:, 0, :], op=ALU.subtract),
                 lambda: nc.vector.tensor_scalar(
-                    out=sign[:, 1, :], in0=y[:], scalar1=0.0, scalar2=0.5, op0=ALU.is_lt, op1=ALU.subtract
-                ),
-                lambda: nc.vector.tensor_scalar(
-                    out=sign[:, 0, :], in0=sign[:, 1, :], scalar1=-1.0, scalar2=None, op0=ALU.mult
+                    out=sign[:], in0=y[:], scalar1=0.0, scalar2=0.5, op0=ALU.is_lt, op1=ALU.subtract
                 ),
             ]
 
@@ -227,11 +225,11 @@ def tile_bsplinekanlayer_s_kernel(tc, x, spline_parameters, w_b, w_s, out):
             inner_s = evals.tile([P, 2 * n], BF16)
             value = evals.tile([P, 2, 2 * n], BF16)
             value_of[c] = value
-            sign = sign_of[c]
+            sign = sign_of[c][:].unsqueeze(1).to_broadcast([P, 2, n])
             return [
-                lambda: nc.vector.tensor_tensor(out=edge_s[:], in0=edge_of[c][:], in1=sign[:], op=ALU.mult),
+                lambda: nc.vector.tensor_tensor(out=edge_s[:], in0=edge_of[c][:], in1=sign, op=ALU.mult),
                 lambda: nc.vector.tensor_tensor(
-                    out=woven(outer_s[:]), in0=halves(outer_of[c][:]), in1=halves(sign[:]), op=ALU.mult
+                    out=woven(outer_s[:]), in0=halves(outer_of[c][:]), in1=halves(sign), op=ALU.mult
                 ),
                 lambda: nc.vector.tensor_tensor(
                     out=woven(inner_s[:]), in0=halves(inner_of[c][:]), in1=halves(edge_s[:]), op=ALU.mult
@@ -352,54 +350,63 @@ def tile_bsplinekanlayer_s_kernel(tc, x, spline_parameters, w_b, w_s, out):
         run(par[0:2])
         run(loc[0:1])
         run(par[2:4])
+        widen_gains()
         run(loc[1:2])
         run(sq[0:1])
+        run(sq[1:8])
         run(loc1[0:1])
-        weave(loc[2:4], hit[0:2])
+        run(par[4:5])
+        run(hit[0:2])
+        run(loc[2:3])
         run(hit[2:4])
         run(loc1[1:2])
-        run(pos2[0:1])
-        run(sq[1:8])
-        regroup_parameters()
-        run(loc1[2:3])
-        run(hit1[0:1])
-        run(loc1[3:4])
         run(sq1[0:1])
-        run(pos2[1:2])
+        run(hit1[0:1])
+        run(pos2)
+        run(loc1[2:3])
+        run(hit1[1:2])
         run(sq1[1:8])
+        regroup_parameters()
+        run(comb[0:2])
         quantise_parameters()
-        weave(comb[0:2], hit1[1:2])
-        weave(comb[2:4], hit1[2:3])
-        run(comb[4:5])
-        run(hit1[3:4])
-        weave(place(0, 0), loc2[0:3])
+        run(comb[2:3])
+        run(hit1[2:4])
+        run(comb[3:5])
+        run(loc2[0:1])
+        weave(place(0, 0), loc2[1:3])
         silu_terms()
         regroup(0)
         run(sq2)
-        sum_silu()
-        widen_gains()
-        run(loc2[3:4])
+        sum_silu(range(0, 3))
         run(hit2[0:1])
         run(comb1[0:3])
-        run(hit2[1:2])
+        run(hit2[1:3])
         run(comb1[3:5])
-        run(hit2[2:3])
-        extra = {1: hit2[3:4], 2: [base_path] + comb2[0:1], 3: comb2[1:5]}
+        run(hit2[3:4])
+        extra = {3: comb2}
         chunk = 0
         for p in range(1, parts):
             if PARTS[p] == CHUNKS[chunk][1]:
                 chunk += 1
             weave(place(chunk, p), extra.get(p, []))
+            if p == 1:
+                sum_silu(range(3, ROWS // SHARE))
             regroup(p)
             if 2 <= p < parts - 3:
                 multiply(p - 2)
+            if p == 3:
+                base_path()
+                for done in range(p - 1):
+                    finish(done, "scalar")
+            elif 3 < p < parts - 3:
                 finish(p - 2, "scalar")
-        for p in range(parts - 5, parts - 2):
-            multiply(p)
-        finish(parts - 5, "vector")
-        finish(parts - 4, "scalar")
-        multiply(parts - 2)
-        finish(parts - 3, "scalar")
-        multiply(parts - 1)
-        finish(parts - 2, "scalar")
-        finish(parts - 1, "vector")
+        multiply(3)
+        multiply(4)
+        multiply(5)
+        finish(3, "vector")
+        finish(4, "scalar")
+        multiply(6)
+        finish(5, "scalar")
+        multiply(7)
+        finish(6, "scalar")
+        finish(7, "vector")

@@ -32,9 +32,9 @@ def tile_bsplinekanlayer_s_kernel(tc, x, spline_parameters, w_b, w_s, out):
 
     with ExitStack() as ctx:
         keep = ctx.enter_context(tc.tile_pool(name="keep", bufs=1))
-        evals = ctx.enter_context(tc.tile_pool(name="evals", bufs=3))
+        evals = ctx.enter_context(tc.tile_pool(name="evals", bufs=len(CHUNKS)))
         work = ctx.enter_context(tc.tile_pool(name="work", bufs=5))
-        results = ctx.enter_context(tc.tile_pool(name="results", bufs=5))
+        results = ctx.enter_context(tc.tile_pool(name="results", bufs=len(PARTS) - 1))
         psum_words = ctx.enter_context(tc.psum_pool(name="psum_words", bufs=4))
         psum_acc = ctx.enter_context(tc.psum_pool(name="psum_acc", bufs=4))
         ctx.enter_context(tc.manual_schedule())
@@ -61,13 +61,13 @@ def tile_bsplinekanlayer_s_kernel(tc, x, spline_parameters, w_b, w_s, out):
         ws = keep.tile([P, 1], F32)
         par_codes = keep.tile([P, OUTS], U32, align_bytes=64)
         par_scales = keep.tile([P, OUTS], U8, align_bytes=64)
-        par_t = psum_words.tile([P, 2, OUTS], F32, tag="words")
+        par_t = psum_acc.tile([P, 2, OUTS], F32, tag="acc")
         wb = keep.tile([P, 1], F32)
         row_of = keep.tile([P, SHARE], F32)
         ident_bf = keep.tile([P, P], BF16)
-        x_t = psum_words.tile([P, ROWS // SHARE, P], BF16, tag="words")
+        x_t = psum_acc.tile([P, ROWS // SHARE, P], BF16, tag="acc")
         silu = keep.tile([P, ROWS // SHARE, P], F32)
-        row_sum = psum_words.tile([P, ROWS], F32, tag="words")
+        row_sum = psum_acc.tile([P, ROWS], F32, tag="acc")
 
         def constants():
             masks.make_identity(nc, ident_bf[:])
@@ -93,38 +93,32 @@ def tile_bsplinekanlayer_s_kernel(tc, x, spline_parameters, w_b, w_s, out):
 
         def widen_gains():
             nc.vector.tensor_copy(out=wb[:], in_=wb_bf[:])
-            nc.vector.tensor_copy(out=ws[:], in_=ws_bf[:])
+            nc.vector.tensor_scalar(out=ws[:], in0=ws_bf[:], scalar1=0.5, scalar2=None, op0=ALU.mult)
 
         def base_path():
             nc.vector.tensor_scalar(
                 out=base_term[:], in0=row_sum[:], scalar1=wb[:, 0:1], scalar2=None, op0=ALU.mult
             )
 
-        def transpose_parameters():
-            par_pairs = keep.tile([P, 2 * P * 2], BF16)
-            par_src = par_sb[:].rearrange("o (q l u t v) -> o u q t v l", q=PAIRS, l=2, u=2, t=2, v=4)
-            par_dst = par_pairs[:].rearrange("o (u q t d h l) -> o u d q t h l", u=2, q=PAIRS, t=2, d=2, h=2)
-
-            def pick(u, d):
-                picked = par_src[:, u, :, :, 1:3, :] if d == 0 else par_src[:, u, :, :, 0:4:3, :]
-                nc.vector.tensor_copy(out=par_dst[:, u, d], in_=picked)
-
-            def negate():
-                smaller = par_pairs[:].rearrange("o (a d m) -> o a d m", d=2, m=4)[:, :, 1, :]
-                nc.vector.tensor_scalar(out=smaller, in0=smaller, scalar1=-1.0, scalar2=None, op0=ALU.mult)
-                for u in range(2):
-                    nc.tensor.transpose(
-                        par_t[:, u, :], par_pairs[:].bitcast(F32)[:, u * P : (u + 1) * P], ident[:]
-                    )
-
-            return [lambda u=u, d=d: pick(u, d) for u in range(2) for d in range(2)] + [negate]
-
         par_grouped = keep.tile([P, OUTS * 4], BF16, align_bytes=64)
 
+        def pick_parameters():
+            pairs = keep.tile([P, 2, 2 * P], BF16)
+            par = par_sb[:].rearrange("o (q l g v) -> o q g v l", q=PAIRS, l=2, g=GROUPS)
+
+            def one_plane(d):
+                nc.vector.tensor_copy(
+                    out=pairs[:, d, :].rearrange("o (q g h l) -> o q g h l", q=PAIRS, g=GROUPS, h=2),
+                    in_=par[:, :, :, 1:3, :] if d == 0 else par[:, :, :, 0:4:3, :],
+                )
+                nc.tensor.transpose(par_t[:, d, :], pairs[:, d, :].bitcast(F32), ident[:])
+
+            return [lambda d=d: one_plane(d) for d in range(2)]
+
         def regroup_parameters():
-            nc.vector.tensor_copy(
-                out=par_grouped[:].bitcast(F32).rearrange("p (o u) -> p o u", u=2),
-                in_=par_t[:].rearrange("p u o -> p o u"),
+            nc.scalar.copy(
+                out=par_grouped[:].bitcast(F32).rearrange("p (o d) -> p o d", d=2),
+                in_=par_t[:].rearrange("p d o -> p o d"),
             )
 
         def quantise_parameters():
@@ -165,17 +159,20 @@ def tile_bsplinekanlayer_s_kernel(tc, x, spline_parameters, w_b, w_s, out):
 
         def locate(c):
             n = count_of(c)
-            w = evals.tile([P, 2, n], BF16)
+            w = evals.tile([P, 2 * n], BF16)
             y = evals.tile([P, n], F32)
             sign = evals.tile([P, n], BF16)
             pos = pos_of[c]
             w_of[c], y_of[c], sign_of[c] = w, y, sign
             return [
                 lambda: nc.vector.tensor_scalar(
-                    out=w[:], in0=pos[:], scalar1=ROUND_MAGIC, scalar2=ROUND_MAGIC,
+                    out=woven(w[:]), in0=halves(pos[:]), scalar1=ROUND_MAGIC, scalar2=ROUND_MAGIC,
                     op0=ALU.add, op1=ALU.subtract,
                 ),
-                lambda: nc.vector.tensor_tensor(out=y[:], in0=pos[:, 0, :], in1=w[:, 0, :], op=ALU.subtract),
+                lambda: nc.vector.tensor_tensor(
+                    out=y[:].rearrange("p (a l) -> p a l", l=2), in0=halves(pos[:])[:, :, 0, :],
+                    in1=woven(w[:])[:, :, 0, :], op=ALU.subtract,
+                ),
                 lambda: nc.vector.tensor_scalar(
                     out=sign[:], in0=y[:], scalar1=0.0, scalar2=0.5, op0=ALU.is_lt, op1=ALU.subtract
                 ),
@@ -187,8 +184,7 @@ def tile_bsplinekanlayer_s_kernel(tc, x, spline_parameters, w_b, w_s, out):
 
             def one_group(g):
                 nc.vector.tensor_scalar(
-                    out=woven(hit[:, g, :]), in0=halves(w_of[c][:]), scalar1=float(g), scalar2=None,
-                    op0=ALU.is_equal,
+                    out=hit[:, g, :], in0=w_of[c][:], scalar1=float(g), scalar2=None, op0=ALU.is_equal
                 )
 
             return [lambda g=g: one_group(g) for g in range(GROUPS)]
@@ -198,9 +194,9 @@ def tile_bsplinekanlayer_s_kernel(tc, x, spline_parameters, w_b, w_s, out):
             dist = evals.tile([P, n], F32)
             ramp = evals.tile([P, 2, n], F32)
             bump = evals.tile([P, 2, n], F32)
-            inner = evals.tile([P, 2, n], BF16)
-            outer = evals.tile([P, 2, n], BF16)
-            edge = evals.tile([P, 2, n], BF16)
+            inner = evals.tile([P, 2 * n], BF16)
+            outer = evals.tile([P, 2 * n], BF16)
+            edge = evals.tile([P, 2 * n], BF16)
             inner_of[c], edge_of[c], outer_of[c] = inner, edge, outer
             y = y_of[c]
 
@@ -211,35 +207,32 @@ def tile_bsplinekanlayer_s_kernel(tc, x, spline_parameters, w_b, w_s, out):
                 act(dist[:], y[:], ACT.Abs, scale=4.0),
                 act(ramp[:, 0, :], dist[:], ACT.Relu, scale=-1.0, bias=1.0),
                 act(ramp[:, 1, :], dist[:], ACT.Relu, scale=1.0, bias=-1.0),
-                act(edge[:, 1, :], ramp[:, 0, :], ACT.Square, scale=-1.0, bias=1.0),
-                act(edge[:, 0, :], ramp[:, 1, :], ACT.Square, scale=-1.0, bias=1.0),
                 act(bump[:], ramp[:], ACT.Square, bias=-0.5),
-                act(outer[:], ramp[:], ACT.Square),
-                act(inner[:], bump[:], ACT.Identity, scale=2.0, bias=-1.5),
+                act(woven(edge[:]), halves(ramp[:, ::-1, :]), ACT.Square, scale=-1.0, bias=1.0),
+                act(woven(inner[:]), halves(bump[:]), ACT.Identity, scale=4.0, bias=-3.0),
+                act(woven(outer[:]), halves(ramp[:]), ACT.Square),
             ]
 
         def combine(c):
             n = count_of(c)
-            edge_s = evals.tile([P, 2, n], BF16)
-            outer_s = evals.tile([P, 2 * n], BF16)
+            edge_s = evals.tile([P, 2 * n], BF16)
             inner_s = evals.tile([P, 2 * n], BF16)
+            inner_m = evals.tile([P, 2 * n], BF16)
             value = evals.tile([P, 2, 2 * n], BF16)
             value_of[c] = value
-            sign = sign_of[c][:].unsqueeze(1).to_broadcast([P, 2, n])
+            signs = sign_of[c][:].rearrange("p (a l) -> p a l", l=2).unsqueeze(2).to_broadcast([P, n // 2, 2, 2])
+
+            def both(out, in0, in1, op):
+                return lambda: nc.vector.tensor_tensor(out=out, in0=in0, in1=in1, op=op)
+
             return [
-                lambda: nc.vector.tensor_tensor(out=edge_s[:], in0=edge_of[c][:], in1=sign, op=ALU.mult),
-                lambda: nc.vector.tensor_tensor(
-                    out=woven(outer_s[:]), in0=halves(outer_of[c][:]), in1=halves(sign), op=ALU.mult
+                both(woven(edge_s[:]), woven(edge_of[c][:]), signs, ALU.mult),
+                both(inner_s[:], inner_of[c][:], edge_s[:], ALU.mult),
+                lambda: nc.vector.tensor_scalar(
+                    out=inner_m[:], in0=inner_s[:], scalar1=-1.0, scalar2=None, op0=ALU.mult
                 ),
-                lambda: nc.vector.tensor_tensor(
-                    out=woven(inner_s[:]), in0=halves(inner_of[c][:]), in1=halves(edge_s[:]), op=ALU.mult
-                ),
-                lambda: nc.vector.tensor_tensor(
-                    out=value[:, 0, :], in0=inner_s[:], in1=outer_s[:], op=ALU.max
-                ),
-                lambda: nc.vector.tensor_tensor(
-                    out=value[:, 1, :], in0=inner_s[:], in1=outer_s[:], op=ALU.min
-                ),
+                both(value[:, 0, :], inner_s[:], outer_of[c][:], ALU.max),
+                both(value[:, 1, :], inner_m[:], outer_of[c][:], ALU.max),
             ]
 
         words_of, grouped_of, acc_of = {}, {}, {}
@@ -251,37 +244,35 @@ def tile_bsplinekanlayer_s_kernel(tc, x, spline_parameters, w_b, w_s, out):
             rows = rows_of(p)
             first = (PARTS[p] - CHUNKS[c][0]) * 2 * FEATURES
             cols = slice(first, first + rows * 2 * FEATURES)
-            shape = [P, rows * PAIRS, 2, 2, 2]
+            shape = [P, rows * PAIRS, GROUPS, 4]
             bases = work.tile([P, 2, rows * 2 * P], BF16)
-            value = value_of[c][:, :, cols].rearrange("p e (a h l) -> p a e h l", h=2, l=2)
             banks = [psum_words.tile([P, 2, 2 * P], F32, name="words") for g in range(rows // 2)]
             words_of[p] = banks
 
-            def one_group(u, t):
+            def one_plane(d):
                 nc.vector.tensor_tensor(
-                    out=bases[:, u, :].rearrange("p (a t e h l) -> p t a e h l", t=2, e=2, h=2, l=2)[:, t],
-                    in0=woven(hit_of[c][:, 2 * u + t, cols]).unsqueeze(2).to_broadcast(shape),
-                    in1=value,
+                    out=bases[:, d, :].rearrange("p (a g m) -> p a g m", g=GROUPS, m=4),
+                    in0=hit_of[c][:, :, cols].rearrange("p g (a m) -> p a g m", m=4),
+                    in1=value_of[c][:, d, cols].rearrange("p (a m) -> p a m", m=4).unsqueeze(2).to_broadcast(shape),
                     op=ALU.mult,
                 )
-                if t == 1:
-                    for row in range(rows):
-                        nc.tensor.transpose(
-                            banks[row // 2][:, u, (row % 2) * P : (row % 2 + 1) * P],
-                            bases[:, u, :].bitcast(F32)[:, row * P : (row + 1) * P],
-                            ident[:],
-                        )
+                for row in range(rows):
+                    nc.tensor.transpose(
+                        banks[row // 2][:, d, (row % 2) * P : (row % 2 + 1) * P],
+                        bases[:, d, :].bitcast(F32)[:, row * P : (row + 1) * P],
+                        ident[:],
+                    )
 
-            return [lambda u=u, t=t: one_group(u, t) for u in range(2) for t in range(2)]
+            return [lambda d=d: one_plane(d) for d in range(2)]
 
         def regroup(p):
             rows = rows_of(p)
             grouped = work.tile([P, rows * P * 4], BF16, align_bytes=64)
-            grouped_v = grouped[:].bitcast(F32).rearrange("p (b u) -> p b u", u=2)
+            grouped_v = grouped[:].bitcast(F32).rearrange("p (b d) -> p b d", d=2)
             for g in range(rows // 2):
                 nc.scalar.copy(
                     out=grouped_v[:, g * 2 * P : (g + 1) * 2 * P, :],
-                    in_=words_of[p][g][:].rearrange("p u b -> p b u"),
+                    in_=words_of[p][g][:].rearrange("p d b -> p b d"),
                 )
             grouped_of[p] = grouped
 
@@ -290,7 +281,9 @@ def tile_bsplinekanlayer_s_kernel(tc, x, spline_parameters, w_b, w_s, out):
             codes = work.tile([P, rows * P], U32, align_bytes=64)
             scales = work.tile([P, rows * P], U8, align_bytes=64)
             acc = psum_acc.tile([P, rows, OUTS], F32)
-            for g in range(rows // 2):
+            acc_of[p] = acc
+
+            def one_bank(g):
                 cols = slice(g * 2 * P, (g + 1) * 2 * P)
                 nc.vector.quantize_mx(
                     out=codes[:, cols].bitcast(FP8X4),
@@ -308,7 +301,8 @@ def tile_bsplinekanlayer_s_kernel(tc, x, spline_parameters, w_b, w_s, out):
                         start=True,
                         stop=True,
                     )
-            acc_of[p] = acc
+
+            return [lambda g=g: one_bank(g) for g in range(rows // 2)]
 
         def finish(p, engine):
             rows = rows_of(p)
@@ -336,77 +330,97 @@ def tile_bsplinekanlayer_s_kernel(tc, x, spline_parameters, w_b, w_s, out):
                 run(first[i : i + 1])
                 run(second[i : i + 1])
 
-        parts = len(PARTS) - 1
+        parts_of = [[p for p in range(len(PARTS) - 1) if lo <= PARTS[p] < hi] for lo, hi in CHUNKS]
+        chunks = range(len(CHUNKS))
         constants()
-        pos, pos1, pos2 = positions(0), positions(1), positions(2)
-        par = transpose_parameters()
-        loc, loc1, loc2 = locate(0), locate(1), locate(2)
-        sq, sq1, sq2 = squares(0), squares(1), squares(2)
-        hit, hit1, hit2 = hits(0), hits(1), hits(2)
-        comb, comb1, comb2 = combine(0), combine(1), combine(2)
-        run(pos1)
-        run(pos)
+        pos = [positions(c) for c in chunks]
+        loc = [locate(c) for c in chunks]
+        sq = [squares(c) for c in chunks]
+        hit = [hits(c) for c in chunks]
+        comb = [combine(c) for c in chunks]
+        run(pos[1])
+        run(pos[0])
         transpose_x()
-        run(par[0:2])
-        run(loc[0:1])
-        run(par[2:4])
-        widen_gains()
-        run(loc[1:2])
-        run(sq[0:1])
-        run(sq[1:8])
-        run(loc1[0:1])
-        run(par[4:5])
-        run(hit[0:2])
-        run(loc[2:3])
-        run(hit[2:4])
-        run(loc1[1:2])
-        run(sq1[0:1])
-        run(hit1[0:1])
-        run(pos2)
-        run(loc1[2:3])
-        run(hit1[1:2])
-        run(sq1[1:8])
-        regroup_parameters()
-        run(comb[0:2])
-        quantise_parameters()
-        run(comb[2:3])
-        run(hit1[2:4])
-        run(comb[3:5])
-        run(loc2[0:1])
-        weave(place(0, 0), loc2[1:3])
+        run(pos[2][0:1])
+        run(loc[0][0:1])
+        pick = pick_parameters()
+        run(pick[0:1])
+        run(loc[0][1:2])
+        run(sq[0][0:1])
         silu_terms()
+        run(pos[2][1:2])
+        run(loc[1][0:1])
+        run(hit[0][0:1])
+        run(loc[1][1:2])
+        run(sq[0][1:3])
+        run(sq[1][0:1])
+        run(sq[0][3:6])
+        run(pick[1:2])
+        sum_silu(range(ROWS // SHARE))
+        run(loc[0][2:3])
+        run(hit[0][1:2])
+        run(loc[2][0:1])
+        run(hit[1][0:1])
+        run(sq[1][1:3])
+        run(sq[0][6:7])
+        run(sq[1][3:6])
+        run(loc[2][1:2])
+        run(hit[1][1:2])
+        run(comb[0][0:1])
+        run(hit[1][2:4])
+        run(comb[0][1:2])
+        run(hit[2][0:1])
+        run(hit[0][2:4])
+        run(comb[0][2:4])
+        run(loc[1][2:3])
+        run(comb[0][4:5])
+        run(hit[2][1:2])
+        run(loc[2][2:3])
+        run(place(0, 0))
+        run(sq[2][0:1])
+        run(sq[1][6:7])
+        run(sq[2][1:3])
+        regroup_parameters()
         regroup(0)
-        run(sq2)
-        sum_silu(range(0, 3))
-        run(hit2[0:1])
-        run(comb1[0:3])
-        run(hit2[1:3])
-        run(comb1[3:5])
-        run(hit2[3:4])
-        extra = {3: comb2}
-        chunk = 0
-        for p in range(1, parts):
-            if PARTS[p] == CHUNKS[chunk][1]:
-                chunk += 1
-            weave(place(chunk, p), extra.get(p, []))
-            if p == 1:
-                sum_silu(range(3, ROWS // SHARE))
-            regroup(p)
-            if 2 <= p < parts - 3:
-                multiply(p - 2)
-            if p == 3:
-                base_path()
-                for done in range(p - 1):
-                    finish(done, "scalar")
-            elif 3 < p < parts - 3:
-                finish(p - 2, "scalar")
-        multiply(3)
-        multiply(4)
-        multiply(5)
+        run(sq[2][3:7])
+        run(comb[1][0:1])
+        run(hit[2][2:3])
+        run(comb[1][1:2])
+        run(hit[2][3:4])
+        run(comb[1][2:5])
+        run(place(1, 1))
+        regroup(1)
+        run(place(1, 2))
+        quantise_parameters()
+        widen_gains()
+        run(multiply(0))
+        regroup(2)
+        run(comb[2][0:1])
+        run(place(1, 3))
+        base_path()
+        run(comb[2][1:2])
+        run(comb[2][2:5])
+        regroup(3)
+        run(place(2, 4))
+        run(multiply(1))
+        finish(0, "scalar")
+        regroup(4)
+        run(multiply(2))
+        run(place(2, 5))
+        finish(1, "scalar")
+        run(place(2, 6))
+        regroup(5)
+        run(multiply(3))
+        run(place(2, 7))
+        regroup(6)
+        run(multiply(4))
+        finish(2, "scalar")
+        run(multiply(5))
+        regroup(7)
         finish(3, "vector")
-        finish(4, "scalar")
-        multiply(6)
-        finish(5, "scalar")
-        multiply(7)
+        run(multiply(6))
+        finish(4, "vector")
+        run(multiply(7))
+        finish(5, "vector")
         finish(6, "scalar")
         finish(7, "vector")

@@ -39,12 +39,11 @@ def tile_bsplinekanlayer_s_kernel(tc, x, spline_parameters, w_b, w_s, out):
         psum_acc = ctx.enter_context(tc.psum_pool(name="psum_acc", bufs=4))
         ctx.enter_context(tc.manual_schedule())
 
-        par_sb = keep.tile([P, FEATURES * BASES], BF16)
-        nc.scalar.dma_start(out=par_sb[:], in_=spline_parameters.rearrange("o i k -> o (i k)"))
         x_sb = keep.tile([P, ROWS, FEATURES], BF16)
-        first = CHUNKS[1][1]
-        nc.sync.dma_start(out=x_sb[:, 0:first, :], in_=x_rows[:, 0:first, :])
-        nc.sync.dma_start(out=x_sb[:, first:ROWS, :], in_=x_rows[:, first:ROWS, :])
+        for (lo, hi), queue in zip(CHUNKS, (nc.sync, nc.scalar, nc.sync)):
+            queue.dma_start(out=x_sb[:, lo:hi, :], in_=x_rows[:, lo:hi, :])
+        par_sb = keep.tile([P, FEATURES * BASES], BF16)
+        nc.sync.dma_start(out=par_sb[:], in_=spline_parameters.rearrange("o i k -> o (i k)"))
         wb_bf = keep.tile([P, 1], BF16)
         nc.sync.dma_start(out=wb_bf[:], in_=w_b.partition_broadcast(P))
         ws_bf = keep.tile([P, 1], BF16)
@@ -240,13 +239,16 @@ def tile_bsplinekanlayer_s_kernel(tc, x, spline_parameters, w_b, w_s, out):
         def rows_of(p):
             return PARTS[p + 1] - PARTS[p]
 
+        def banks_of(p):
+            return [(row, min(2, rows_of(p) - row)) for row in range(0, rows_of(p), 2)]
+
         def place(c, p):
             rows = rows_of(p)
             first = (PARTS[p] - CHUNKS[c][0]) * 2 * FEATURES
             cols = slice(first, first + rows * 2 * FEATURES)
             shape = [P, rows * PAIRS, GROUPS, 4]
             bases = work.tile([P, 2, rows * 2 * P], BF16)
-            banks = [psum_words.tile([P, 2, 2 * P], F32, name="words") for g in range(rows // 2)]
+            banks = [psum_words.tile([P, 2, 2 * P], F32, name="words") for bank in banks_of(p)]
             words_of[p] = banks
 
             def one_plane(d):
@@ -269,10 +271,10 @@ def tile_bsplinekanlayer_s_kernel(tc, x, spline_parameters, w_b, w_s, out):
             rows = rows_of(p)
             grouped = work.tile([P, rows * P * 4], BF16, align_bytes=64)
             grouped_v = grouped[:].bitcast(F32).rearrange("p (b d) -> p b d", d=2)
-            for g in range(rows // 2):
+            for (first, some), words in zip(banks_of(p), words_of[p]):
                 nc.scalar.copy(
-                    out=grouped_v[:, g * 2 * P : (g + 1) * 2 * P, :],
-                    in_=words_of[p][g][:].rearrange("p d b -> p b d"),
+                    out=grouped_v[:, first * P : (first + some) * P, :],
+                    in_=words[:, :, 0 : some * P].rearrange("p d b -> p b d"),
                 )
             grouped_of[p] = grouped
 
@@ -283,14 +285,14 @@ def tile_bsplinekanlayer_s_kernel(tc, x, spline_parameters, w_b, w_s, out):
             acc = psum_acc.tile([P, rows, OUTS], F32)
             acc_of[p] = acc
 
-            def one_bank(g):
-                cols = slice(g * 2 * P, (g + 1) * 2 * P)
+            def one_bank(first, some):
+                cols = slice(first * P, (first + some) * P)
                 nc.vector.quantize_mx(
                     out=codes[:, cols].bitcast(FP8X4),
                     scales=scales[:, cols],
-                    in_=grouped_of[p][:, g * 8 * P : (g + 1) * 8 * P],
+                    in_=grouped_of[p][:, first * 4 * P : (first + some) * 4 * P],
                 )
-                for row in range(2 * g, 2 * g + 2):
+                for row in range(first, first + some):
                     cols = slice(row * P, (row + 1) * P)
                     nc.tensor.matmul_mx(
                         out=acc[:, row, :],
@@ -302,7 +304,7 @@ def tile_bsplinekanlayer_s_kernel(tc, x, spline_parameters, w_b, w_s, out):
                         stop=True,
                     )
 
-            return [lambda g=g: one_bank(g) for g in range(rows // 2)]
+            return [lambda bank=bank: one_bank(*bank) for bank in banks_of(p)]
 
         def finish(p, engine):
             rows = rows_of(p)
@@ -343,19 +345,17 @@ def tile_bsplinekanlayer_s_kernel(tc, x, spline_parameters, w_b, w_s, out):
         transpose_x()
         run(pos[2][0:1])
         run(loc[0][0:1])
-        pick = pick_parameters()
-        run(pick[0:1])
+        run(pos[2][1:2])
         run(loc[0][1:2])
         run(sq[0][0:1])
         silu_terms()
-        run(pos[2][1:2])
         run(loc[1][0:1])
         run(hit[0][0:1])
         run(loc[1][1:2])
         run(sq[0][1:3])
         run(sq[1][0:1])
         run(sq[0][3:6])
-        run(pick[1:2])
+        run(pick_parameters())
         sum_silu(range(ROWS // SHARE))
         run(loc[0][2:3])
         run(hit[0][1:2])
@@ -399,10 +399,12 @@ def tile_bsplinekanlayer_s_kernel(tc, x, spline_parameters, w_b, w_s, out):
         run(place(1, 3))
         base_path()
         run(comb[2][1:2])
+        mul1 = multiply(1)
+        run(mul1[0:1])
         run(comb[2][2:5])
         regroup(3)
         run(place(2, 4))
-        run(multiply(1))
+        run(mul1[1:2])
         finish(0, "scalar")
         regroup(4)
         run(multiply(2))
@@ -419,7 +421,7 @@ def tile_bsplinekanlayer_s_kernel(tc, x, spline_parameters, w_b, w_s, out):
         regroup(7)
         finish(3, "vector")
         run(multiply(6))
-        finish(4, "vector")
+        finish(4, "scalar")
         run(multiply(7))
         finish(5, "vector")
         finish(6, "scalar")

@@ -35,8 +35,8 @@ def tile_bsplinekanlayer_s_kernel(tc, x, spline_parameters, w_b, w_s, out):
         evals = ctx.enter_context(tc.tile_pool(name="evals", bufs=len(CHUNKS)))
         work = ctx.enter_context(tc.tile_pool(name="work", bufs=5))
         results = ctx.enter_context(tc.tile_pool(name="results", bufs=len(PARTS) - 1))
-        psum_words = ctx.enter_context(tc.psum_pool(name="psum_words", bufs=4))
-        psum_acc = ctx.enter_context(tc.psum_pool(name="psum_acc", bufs=4))
+        psum_words = ctx.enter_context(tc.psum_pool(name="psum_words", bufs=5))
+        psum_acc = ctx.enter_context(tc.psum_pool(name="psum_acc", bufs=3))
         ctx.enter_context(tc.manual_schedule())
 
         x_sb = keep.tile([P, ROWS, FEATURES], BF16)
@@ -351,11 +351,11 @@ def tile_bsplinekanlayer_s_kernel(tc, x, spline_parameters, w_b, w_s, out):
         silu_terms()
         run(loc[1][0:1])
         run(hit[0][0:1])
+        run(pick_parameters())
         run(loc[1][1:2])
         run(sq[0][1:3])
         run(sq[1][0:1])
         run(sq[0][3:6])
-        run(pick_parameters())
         sum_silu(range(ROWS // SHARE))
         run(loc[0][2:3])
         run(hit[0][1:2])
@@ -381,8 +381,9 @@ def tile_bsplinekanlayer_s_kernel(tc, x, spline_parameters, w_b, w_s, out):
         run(sq[1][6:7])
         run(sq[2][1:3])
         regroup_parameters()
+        run(sq[2][3:5])
         regroup(0)
-        run(sq[2][3:7])
+        run(sq[2][5:7])
         run(comb[1][0:1])
         run(hit[2][2:3])
         run(comb[1][1:2])
@@ -392,37 +393,37 @@ def tile_bsplinekanlayer_s_kernel(tc, x, spline_parameters, w_b, w_s, out):
         regroup(1)
         run(place(1, 2))
         quantise_parameters()
-        widen_gains()
-        run(multiply(0))
-        regroup(2)
         run(comb[2][0:1])
+        widen_gains()
         run(place(1, 3))
         base_path()
+        mul0 = multiply(0)
+        run(mul0[0:1])
+        regroup(2)
         run(comb[2][1:2])
-        mul1 = multiply(1)
-        run(mul1[0:1])
+        run(mul0[1:2])
         run(comb[2][2:5])
         regroup(3)
         run(place(2, 4))
-        run(mul1[1:2])
+        run(multiply(1))
         finish(0, "scalar")
         regroup(4)
         run(multiply(2))
         run(place(2, 5))
         finish(1, "scalar")
         run(place(2, 6))
+        run(place(2, 7))
         regroup(5)
         run(multiply(3))
-        run(place(2, 7))
         regroup(6)
         run(multiply(4))
-        finish(2, "scalar")
-        run(multiply(5))
         regroup(7)
+        finish(2, "vector")
+        run(multiply(5))
         finish(3, "vector")
-        run(multiply(6))
         finish(4, "scalar")
+        run(multiply(6))
         run(multiply(7))
-        finish(5, "vector")
+        finish(5, "scalar")
         finish(6, "scalar")
         finish(7, "vector")

@@ -80,8 +80,8 @@ def tile_bsplinekanlayer_s_kernel(tc, x, spline_parameters, w_b, w_s, out):
                     x_t[:, g, :], x_sb[:, g * SHARE : (g + 1) * SHARE, :].rearrange("p t i -> p (t i)"), ident_bf[:]
                 )
 
-        def silu_terms():
-            nc.scalar.activation(out=silu[:], in_=x_t[:], func=ACT.Silu)
+        def silu_terms(lo, hi):
+            nc.scalar.activation(out=silu[:, lo:hi, :], in_=x_t[:, lo:hi, :], func=ACT.Silu)
 
         def sum_silu(shares):
             for g in shares:
@@ -91,8 +91,8 @@ def tile_bsplinekanlayer_s_kernel(tc, x, spline_parameters, w_b, w_s, out):
                 )
 
         def widen_gains():
-            nc.vector.tensor_copy(out=wb[:], in_=wb_bf[:])
-            nc.vector.tensor_scalar(out=ws[:], in0=ws_bf[:], scalar1=0.5, scalar2=None, op0=ALU.mult)
+            nc.gpsimd.tensor_copy(out=wb[:], in_=wb_bf[:])
+            nc.gpsimd.tensor_scalar(out=ws[:], in0=ws_bf[:], scalar1=0.5, scalar2=None, op0=ALU.mult)
 
         def base_path():
             nc.vector.tensor_scalar(
@@ -205,7 +205,11 @@ def tile_bsplinekanlayer_s_kernel(tc, x, spline_parameters, w_b, w_s, out):
             return [
                 act(dist[:], y[:], ACT.Abs, scale=4.0),
                 act(ramp[:, 0, :], dist[:], ACT.Relu, scale=-1.0, bias=1.0),
-                act(ramp[:, 1, :], dist[:], ACT.Relu, scale=1.0, bias=-1.0),
+                lambda: nc.vector.tensor_scalar(
+                    out=ramp[:, 1, :], in0=dist[:], scalar1=-1.0, scalar2=0.0, op0=ALU.add, op1=ALU.max
+                ) if c > 0 else nc.scalar.activation(
+                    out=ramp[:, 1, :], in_=dist[:], func=ACT.Relu, scale=1.0, bias=-1.0
+                ),
                 act(bump[:], ramp[:], ACT.Square, bias=-0.5),
                 act(woven(edge[:]), halves(ramp[:, ::-1, :]), ACT.Square, scale=-1.0, bias=1.0),
                 act(woven(inner[:]), halves(bump[:]), ACT.Identity, scale=4.0, bias=-3.0),
@@ -282,7 +286,10 @@ def tile_bsplinekanlayer_s_kernel(tc, x, spline_parameters, w_b, w_s, out):
             rows = rows_of(p)
             codes = work.tile([P, rows * P], U32, align_bytes=64)
             scales = work.tile([P, rows * P], U8, align_bytes=64)
-            acc = psum_acc.tile([P, rows, OUTS], F32)
+            if p < PARTS.index(ROWS) - 2:
+                acc = psum_acc.tile([P, rows, OUTS], F32)
+            else:
+                acc = psum_words.tile([P, rows, OUTS], F32, tag="words")
             acc_of[p] = acc
 
             def one_bank(first, some):
@@ -343,12 +350,14 @@ def tile_bsplinekanlayer_s_kernel(tc, x, spline_parameters, w_b, w_s, out):
         run(pos[1])
         run(pos[0])
         transpose_x()
+        silu_terms(0, 3)
+        widen_gains()
         run(pos[2][0:1])
         run(loc[0][0:1])
         run(pos[2][1:2])
         run(loc[0][1:2])
         run(sq[0][0:1])
-        silu_terms()
+        silu_terms(3, ROWS // SHARE)
         run(loc[1][0:1])
         run(hit[0][0:1])
         run(pick_parameters())
@@ -361,11 +370,12 @@ def tile_bsplinekanlayer_s_kernel(tc, x, spline_parameters, w_b, w_s, out):
         run(hit[0][1:2])
         run(loc[2][0:1])
         run(hit[1][0:1])
-        run(sq[1][1:3])
-        run(sq[0][6:7])
-        run(sq[1][3:6])
         run(loc[2][1:2])
         run(hit[1][1:2])
+        run(sq[1][1:3])
+        run(sq[0][6:7])
+        run(sq[2][0:1])
+        run(sq[1][3:6])
         run(comb[0][0:1])
         run(hit[1][2:4])
         run(comb[0][1:2])
@@ -376,10 +386,9 @@ def tile_bsplinekanlayer_s_kernel(tc, x, spline_parameters, w_b, w_s, out):
         run(comb[0][4:5])
         run(hit[2][1:2])
         run(loc[2][2:3])
-        run(place(0, 0))
-        run(sq[2][0:1])
-        run(sq[1][6:7])
         run(sq[2][1:3])
+        run(sq[1][6:7])
+        run(place(0, 0))
         regroup_parameters()
         run(sq[2][3:5])
         regroup(0)
@@ -394,7 +403,6 @@ def tile_bsplinekanlayer_s_kernel(tc, x, spline_parameters, w_b, w_s, out):
         run(place(1, 2))
         quantise_parameters()
         run(comb[2][0:1])
-        widen_gains()
         run(place(1, 3))
         base_path()
         mul0 = multiply(0)
@@ -413,12 +421,12 @@ def tile_bsplinekanlayer_s_kernel(tc, x, spline_parameters, w_b, w_s, out):
         finish(1, "scalar")
         run(place(2, 6))
         run(place(2, 7))
+        finish(2, "scalar")
         regroup(5)
         run(multiply(3))
         regroup(6)
         run(multiply(4))
         regroup(7)
-        finish(2, "vector")
         run(multiply(5))
         finish(3, "vector")
         finish(4, "scalar")

from contextlib import ExitStack

import concourse.masks as masks
import concourse.mybir as mybir

F32 = mybir.dt.float32
BF16 = mybir.dt.bfloat16
U32 = mybir.dt.uint32
U8 = mybir.dt.uint8
FP8X4 = mybir.dt.float8_e4m3fn_x4
ACT = mybir.ActivationFunctionType
ALU = mybir.AluOpType

P = 128
BATCH, FEATURES, OUTS, BASES = 3584, 32, 128, 16
ROWS = BATCH // P
PAIRS = FEATURES // 2
SHARE = P // FEATURES
GROUPS = 4
PARTS = (0, 4, 8, 12, 16, 20, 24, 26, 28)
CHUNKS = ((0, 4), (4, 16), (16, 28))
KNOTS_PER_UNIT = 57.0 / 7.0
ROUND_MAGIC = 12582912.0

FLOPS = 2 * BATCH * FEATURES * BASES * OUTS


def tile_bsplinekanlayer_s_kernel(tc, x, spline_parameters, w_b, w_s, out):
    nc = tc.nc
    x_rows = x.rearrange("(p t) i -> p t i", t=ROWS)
    out_rows = out.rearrange("(p t) o -> p t o", t=ROWS)

    with ExitStack() as ctx:
        keep = ctx.enter_context(tc.tile_pool(name="keep", bufs=1))
        evals = ctx.enter_context(tc.tile_pool(name="evals", bufs=len(CHUNKS)))
        work = ctx.enter_context(tc.tile_pool(name="work", bufs=5))
        results = ctx.enter_context(tc.tile_pool(name="results", bufs=len(PARTS) - 1))
        psum_words = ctx.enter_context(tc.psum_pool(name="psum_words", bufs=5))
        psum_acc = ctx.enter_context(tc.psum_pool(name="psum_acc", bufs=3))
        ctx.enter_context(tc.manual_schedule())

        x_sb = keep.tile([P, ROWS, FEATURES], BF16)
        for (lo, hi), queue in zip(CHUNKS, (nc.sync, nc.scalar, nc.sync)):
            queue.dma_start(out=x_sb[:, lo:hi, :], in_=x_rows[:, lo:hi, :])
        par_sb = keep.tile([P, FEATURES * BASES], BF16)
        nc.sync.dma_start(out=par_sb[:], in_=spline_parameters.rearrange("o i k -> o (i k)"))
        wb_bf = keep.tile([P, 1], BF16)
        nc.sync.dma_start(out=wb_bf[:], in_=w_b.partition_broadcast(P))
        ws_bf = keep.tile([P, 1], BF16)
        nc.sync.dma_start(out=ws_bf[:], in_=w_s.partition_broadcast(P))

        ident = keep.tile([P, P], F32)
        masks.make_identity(nc, ident[:])

        warm = keep.tile([P, 1], F32)
        nc.vector.memset(warm[:], 0.0)
        nc.scalar.activation(out=warm[:], in_=warm[:], func=ACT.Silu)

        base_term = keep.tile([P, ROWS], F32)
        ws = keep.tile([P, 1], F32)
        par_codes = keep.tile([P, OUTS], U32, align_bytes=64)
        par_scales = keep.tile([P, OUTS], U8, align_bytes=64)
        par_t = psum_acc.tile([P, 2, OUTS], F32, tag="acc")
        wb = keep.tile([P, 1], F32)
        row_of = keep.tile([P, SHARE], F32)
        ident_bf = keep.tile([P, P], BF16)
        x_t = psum_acc.tile([P, ROWS // SHARE, P], BF16, tag="acc")
        silu = keep.tile([P, ROWS // SHARE, P], F32)
        row_sum = psum_acc.tile([P, ROWS], F32, tag="acc")

        def constants():
            masks.make_identity(nc, ident_bf[:])
            nc.gpsimd.memset(row_of[:], 0.0)
            for r in range(SHARE):
                nc.gpsimd.memset(row_of[r * FEATURES : (r + 1) * FEATURES, r : r + 1], 1.0)

        def transpose_x():
            for g in range(ROWS // SHARE):
                nc.tensor.transpose(
                    x_t[:, g, :], x_sb[:, g * SHARE : (g + 1) * SHARE, :].rearrange("p t i -> p (t i)"), ident_bf[:]
                )

        def silu_terms(lo, hi):
            nc.scalar.activation(out=silu[:, lo:hi, :], in_=x_t[:, lo:hi, :], func=ACT.Silu)

        def sum_silu(shares):
            for g in shares:
                nc.tensor.matmul(
                    out=row_sum[:, g * SHARE : (g + 1) * SHARE], lhsT=silu[:, g, :], rhs=row_of[:],
                    start=True, stop=True,
                )

        def widen_gains():
            nc.gpsimd.tensor_copy(out=wb[:], in_=wb_bf[:])
            nc.gpsimd.tensor_scalar(out=ws[:], in0=ws_bf[:], scalar1=0.5, scalar2=None, op0=ALU.mult)

        def base_path():
            nc.vector.tensor_scalar(
                out=base_term[:], in0=row_sum[:], scalar1=wb[:, 0:1], scalar2=None, op0=ALU.mult
            )

        par_grouped = keep.tile([P, OUTS * 4], BF16, align_bytes=64)

        def pick_parameters():
            pairs = keep.tile([P, 2, 2 * P], BF16)
            par = par_sb[:].rearrange("o (q l g v) -> o q g v l", q=PAIRS, l=2, g=GROUPS)

            def one_plane(d):
                nc.vector.tensor_copy(
                    out=pairs[:, d, :].rearrange("o (q g h l) -> o q g h l", q=PAIRS, g=GROUPS, h=2),
                    in_=par[:, :, :, 1:3, :] if d == 0 else par[:, :, :, 0:4:3, :],
                )
                nc.tensor.transpose(par_t[:, d, :], pairs[:, d, :].bitcast(F32), ident[:])

            return [lambda d=d: one_plane(d) for d in range(2)]

        def regroup_parameters():
            nc.scalar.copy(
                out=par_grouped[:].bitcast(F32).rearrange("p (o d) -> p o d", d=2),
                in_=par_t[:].rearrange("p d o -> p o d"),
            )

        def quantise_parameters():
            nc.vector.quantize_mx(
                out=par_codes[:].bitcast(FP8X4), scales=par_scales[:], in_=par_grouped[:]
            )

        pos_of, w_of, y_of, sign_of, dist_of = {}, {}, {}, {}, {}
        inner_of, edge_of, outer_of, value_of, hit_of = {}, {}, {}, {}, {}

        def count_of(c):
            return (CHUNKS[c][1] - CHUNKS[c][0]) * FEATURES

        def halves(planes):
            return planes.rearrange("p h (a l) -> p a h l", l=2)

        def woven(flat):
            return flat.rearrange("p (a h l) -> p a h l", h=2, l=2)

        def positions(c):
            pos = evals.tile([P, 2, count_of(c)], F32)
            pos_of[c] = pos
            lo, hi = CHUNKS[c]

            def one_half(h):
                out = pos[:, h, :].rearrange("p (t i) -> p t i", i=FEATURES)
                scale, bias = KNOTS_PER_UNIT / 4.0, 9.0 / 4.0 - (h + 1) / 2.0
                if c != 1:
                    nc.vector.tensor_scalar(
                        out=out, in0=x_sb[:, lo:hi, :], scalar1=scale, scalar2=bias, op0=ALU.mult, op1=ALU.add
                    )
                else:
                    nc.scalar.activation(
                        out=out, in_=x_sb[:, lo:hi, :], func=ACT.Identity, scale=scale, bias=bias
                    )

            return [lambda: one_half(0), lambda: one_half(1)]

        def locate(c):
            n = count_of(c)
            w = evals.tile([P, 2 * n], BF16)
            y = evals.tile([P, n], F32)
            sign = evals.tile([P, n], BF16)
            pos = pos_of[c]
            w_of[c], y_of[c], sign_of[c] = w, y, sign
            return [
                lambda: nc.vector.tensor_scalar(
                    out=woven(w[:]), in0=halves(pos[:]), scalar1=ROUND_MAGIC, scalar2=ROUND_MAGIC,
                    op0=ALU.add, op1=ALU.subtract,
                ),
                lambda: nc.vector.tensor_tensor(
                    out=y[:].rearrange("p (a l) -> p a l", l=2), in0=halves(pos[:])[:, :, 0, :],
                    in1=woven(w[:])[:, :, 0, :], op=ALU.subtract,
                ),
                lambda: nc.vector.tensor_scalar(
                    out=sign[:], in0=y[:], scalar1=0.0, scalar2=0.5, op0=ALU.is_lt, op1=ALU.subtract
                ),
            ]

        def hits(c):
            hit = evals.tile([P, GROUPS, 2 * count_of(c)], BF16)
            hit_of[c] = hit

            def one_group(g):
                nc.vector.tensor_scalar(
                    out=hit[:, g, :], in0=w_of[c][:], scalar1=float(g), scalar2=None, op0=ALU.is_equal
                )

            return [lambda g=g: one_group(g) for g in range(GROUPS)]

        def squares(c):
            n = count_of(c)
            dist = evals.tile([P, n], F32)
            ramp = evals.tile([P, 2, n], F32)
            bump = evals.tile([P, 2, n], F32)
            inner = evals.tile([P, 2 * n], BF16)
            outer = evals.tile([P, 2 * n], BF16)
            edge = evals.tile([P, 2 * n], BF16)
            inner_of[c], edge_of[c], outer_of[c] = inner, edge, outer
            y = y_of[c]

            def act(out, in_, func, scale=1.0, bias=0.0):
                return lambda: nc.scalar.activation(out=out, in_=in_, func=func, scale=scale, bias=bias)

            return [
                act(dist[:], y[:], ACT.Abs, scale=4.0),
                act(ramp[:, 0, :], dist[:], ACT.Relu, scale=-1.0, bias=1.0),
                lambda: nc.vector.tensor_scalar(
                    out=ramp[:, 1, :], in0=dist[:], scalar1=-1.0, scalar2=0.0, op0=ALU.add, op1=ALU.max
                ) if c > 0 else nc.scalar.activation(
                    out=ramp[:, 1, :], in_=dist[:], func=ACT.Relu, scale=1.0, bias=-1.0
                ),
                act(bump[:], ramp[:], ACT.Square, bias=-0.5),
                act(woven(edge[:]), halves(ramp[:, ::-1, :]), ACT.Square, scale=-1.0, bias=1.0),
                act(woven(inner[:]), halves(bump[:]), ACT.Identity, scale=4.0, bias=-3.0),
                act(woven(outer[:]), halves(ramp[:]), ACT.Square),
            ]

        def combine(c):
            n = count_of(c)
            edge_s = evals.tile([P, 2 * n], BF16)
            inner_s = evals.tile([P, 2 * n], BF16)
            inner_m = evals.tile([P, 2 * n], BF16)
            value = evals.tile([P, 2, 2 * n], BF16)
            value_of[c] = value
            signs = sign_of[c][:].rearrange("p (a l) -> p a l", l=2).unsqueeze(2).to_broadcast([P, n // 2, 2, 2])

            def both(out, in0, in1, op):
                return lambda: nc.vector.tensor_tensor(out=out, in0=in0, in1=in1, op=op)

            return [
                both(woven(edge_s[:]), woven(edge_of[c][:]), signs, ALU.mult),
                both(inner_s[:], inner_of[c][:], edge_s[:], ALU.mult),
                lambda: nc.vector.tensor_scalar(
                    out=inner_m[:], in0=inner_s[:], scalar1=-1.0, scalar2=None, op0=ALU.mult
                ),
                both(value[:, 0, :], inner_s[:], outer_of[c][:], ALU.max),
                both(value[:, 1, :], inner_m[:], outer_of[c][:], ALU.max),
            ]

        words_of, grouped_of, acc_of = {}, {}, {}

        def rows_of(p):
            return PARTS[p + 1] - PARTS[p]

        def banks_of(p):
            return [(row, min(2, rows_of(p) - row)) for row in range(0, rows_of(p), 2)]

        def place(c, p):
            rows = rows_of(p)
            first = (PARTS[p] - CHUNKS[c][0]) * 2 * FEATURES
            cols = slice(first, first + rows * 2 * FEATURES)
            shape = [P, rows * PAIRS, GROUPS, 4]
            bases = work.tile([P, 2, rows * 2 * P], BF16)
            banks = [psum_words.tile([P, 2, 2 * P], F32, name="words") for bank in banks_of(p)]
            words_of[p] = banks

            def one_plane(d):
                nc.vector.tensor_tensor(
                    out=bases[:, d, :].rearrange("p (a g m) -> p a g m", g=GROUPS, m=4),
                    in0=hit_of[c][:, :, cols].rearrange("p g (a m) -> p a g m", m=4),
                    in1=value_of[c][:, d, cols].rearrange("p (a m) -> p a m", m=4).unsqueeze(2).to_broadcast(shape),
                    op=ALU.mult,
                )
                for row in range(rows):
                    nc.tensor.transpose(
                        banks[row // 2][:, d, (row % 2) * P : (row % 2 + 1) * P],
                        bases[:, d, :].bitcast(F32)[:, row * P : (row + 1) * P],
                        ident[:],
                    )

            return [lambda d=d: one_plane(d) for d in range(2)]

        def regroup(p):
            rows = rows_of(p)
            grouped = work.tile([P, rows * P * 4], BF16, align_bytes=64)
            grouped_v = grouped[:].bitcast(F32).rearrange("p (b d) -> p b d", d=2)
            for (first, some), words in zip(banks_of(p), words_of[p]):
                nc.scalar.copy(
                    out=grouped_v[:, first * P : (first + some) * P, :],
                    in_=words[:, :, 0 : some * P].rearrange("p d b -> p b d"),
                )
            grouped_of[p] = grouped

        def multiply(p):
            rows = rows_of(p)
            codes = work.tile([P, rows * P], U32, align_bytes=64)
            scales = work.tile([P, rows * P], U8, align_bytes=64)
            if p < PARTS.index(ROWS) - 2:
                acc = psum_acc.tile([P, rows, OUTS], F32)
            else:
                acc = psum_words.tile([P, rows, OUTS], F32, tag="words")
            acc_of[p] = acc

            def one_bank(first, some):
                cols = slice(first * P, (first + some) * P)
                nc.vector.quantize_mx(
                    out=codes[:, cols].bitcast(FP8X4),
                    scales=scales[:, cols],
                    in_=grouped_of[p][:, first * 4 * P : (first + some) * 4 * P],
                )
                for row in range(first, first + some):
                    cols = slice(row * P, (row + 1) * P)
                    nc.tensor.matmul_mx(
                        out=acc[:, row, :],
                        lhsT=codes[:, cols].bitcast(FP8X4),
                        lhsT_scale=scales[:, cols],
                        rhs=par_codes[:].bitcast(FP8X4),
                        rhs_scale=par_scales[:],
                        start=True,
                        stop=True,
                    )

            return [lambda bank=bank: one_bank(*bank) for bank in banks_of(p)]

        def finish(p, engine):
            rows = rows_of(p)
            result = results.tile([P, rows, OUTS], F32)
            base = base_term[:, PARTS[p] : PARTS[p + 1]]
            if engine == "vector":
                nc.vector.scalar_tensor_tensor(
                    out=result[:], in0=acc_of[p][:], scalar=ws[:, 0:1],
                    in1=base.unsqueeze(2).to_broadcast([P, rows, OUTS]), op0=ALU.mult, op1=ALU.add,
                )
            else:
                for row in range(rows):
                    nc.scalar.activation(
                        out=result[:, row, :], in_=acc_of[p][:, row, :], func=ACT.Identity,
                        scale=ws[:, 0:1], bias=base[:, row : row + 1],
                    )
            nc.sync.dma_start(out=out_rows[:, PARTS[p] : PARTS[p + 1], :], in_=result[:])

        def run(jobs):
            for job in jobs:
                job()

        def weave(first, second):
            for i in range(max(len(first), len(second))):
                run(first[i : i + 1])
                run(second[i : i + 1])

        parts_of = [[p for p in range(len(PARTS) - 1) if lo <= PARTS[p] < hi] for lo, hi in CHUNKS]
        chunks = range(len(CHUNKS))
        constants()
        pos = [positions(c) for c in chunks]
        loc = [locate(c) for c in chunks]
        sq = [squares(c) for c in chunks]
        hit = [hits(c) for c in chunks]
        comb = [combine(c) for c in chunks]
        run(pos[1])
        run(pos[0])
        transpose_x()
        silu_terms(0, 3)
        widen_gains()
        run(pos[2][0:1])
        run(loc[0][0:1])
        run(pos[2][1:2])
        run(loc[0][1:2])
        run(sq[0][0:1])
        silu_terms(3, ROWS // SHARE)
        run(loc[1][0:1])
        run(hit[0][0:1])
        run(pick_parameters())
        run(loc[1][1:2])
        run(sq[0][1:3])
        run(sq[1][0:1])
        run(sq[0][3:6])
        sum_silu(range(ROWS // SHARE))
        run(loc[0][2:3])
        run(hit[0][1:2])
        run(loc[2][0:1])
        run(hit[1][0:1])
        run(loc[2][1:2])
        run(hit[1][1:2])
        run(sq[1][1:3])
        run(sq[0][6:7])
        run(sq[2][0:1])
        run(sq[1][3:6])
        run(comb[0][0:1])
        run(hit[1][2:4])
        run(comb[0][1:2])
        run(hit[2][0:1])
        run(hit[0][2:4])
        run(comb[0][2:4])
        run(loc[1][2:3])
        run(comb[0][4:5])
        run(hit[2][1:2])
        run(loc[2][2:3])
        run(sq[2][1:3])
        run(sq[1][6:7])
        run(place(0, 0))
        regroup_parameters()
        run(sq[2][3:5])
        regroup(0)
        run(sq[2][5:7])
        run(comb[1][0:1])
        run(hit[2][2:3])
        run(comb[1][1:2])
        run(hit[2][3:4])
        run(comb[1][2:5])
        run(place(1, 1))
        regroup(1)
        run(place(1, 2))
        quantise_parameters()
        run(comb[2][0:1])
        run(place(1, 3))
        base_path()
        mul0 = multiply(0)
        run(mul0[0:1])
        regroup(2)
        run(comb[2][1:2])
        run(mul0[1:2])
        run(comb[2][2:5])
        regroup(3)
        run(place(2, 4))
        run(multiply(1))
        finish(0, "scalar")
        regroup(4)
        run(multiply(2))
        run(place(2, 5))
        finish(1, "scalar")
        run(place(2, 6))
        run(place(2, 7))
        finish(2, "scalar")
        regroup(5)
        run(multiply(3))
        regroup(6)
        run(multiply(4))
        regroup(7)
        run(multiply(5))
        finish(3, "vector")
        finish(4, "scalar")
        run(multiply(6))
        run(multiply(7))
        finish(5, "scalar")
        finish(6, "scalar")
        finish(7, "vector")
